import numpy as np
import ml_dtypes


def mxq(x, axis, fmt="e4m3"):
    dtype, down = {"e4m3": (ml_dtypes.float8_e4m3fn, 7), "e5m2": (ml_dtypes.float8_e5m2, 14)}[fmt]
    v = np.moveaxis(np.asarray(x, np.float32).astype(ml_dtypes.bfloat16).astype(np.float64), axis, -1)
    blocks = v.reshape(v.shape[:-1] + (-1, 32))
    amax = np.abs(blocks).max(-1, keepdims=True)
    byte = np.maximum(np.where(amax > 0, np.frexp(amax)[1] - 1 + 127, 0) - down, 1)
    scale = np.exp2(byte - 127.0)
    codes = (blocks / scale).astype(np.float32).astype(dtype).astype(np.float64)
    return np.moveaxis((codes * scale).reshape(v.shape), -1, axis)


WIDE = False


def mx_kscale(k):
    if not WIDE:
        return np.ones(k)
    levels = np.array([10, -10, 5, -5, 0])
    a = np.random.permutation(np.resize(levels, k // 512 * 4)).reshape(k // 512, 4)
    idx = np.arange(k)
    return np.exp2(a[idx // 512, idx % 128 // 32])


BF16 = ml_dtypes.bfloat16


def bf(x):
    return np.asarray(x, np.float32).astype(BF16)


def f64(x):
    return np.asarray(x).astype(np.float64)


E2M1 = np.array([0.0, 0.5, 1.0, 1.5, 2.0, 3.0, 4.0, 6.0, -0.0, -0.5, -1.0, -1.5, -2.0, -3.0, -4.0, -6.0])


def pack_weight(w, fmt):
    k, n = w.shape
    w = f64(bf(w)).reshape(k // 32, 32, n)
    amax = np.abs(w).max(1)
    if fmt == "e4m3":
        byte = np.frexp(amax)[1] - 1 + 127 - 7
    else:
        mant, ex = np.frexp(amax / 6.0)
        byte = np.where(mant > 0.5, ex, ex - 1) + 127
    byte = np.clip(np.where(amax > 0, byte, 1), 1, 254)
    scaled = (w * np.exp2(127.0 - byte)[:, None, :]).reshape(k, n).astype(np.float32)
    by_word = np.ascontiguousarray(scaled.reshape(k // 512, 128, 4, n).transpose(0, 1, 3, 2))
    if fmt == "e4m3":
        words = by_word.astype(ml_dtypes.float8_e4m3fn).view(np.uint8)
    else:
        c = by_word.astype(ml_dtypes.float4_e2m1fn).view(np.uint8) & 0xF
        words = c[..., 0::2] | (c[..., 1::2] << 4)
    return np.ascontiguousarray(words), np.ascontiguousarray(byte.astype(np.uint8).reshape(k // 512, 16, n))


def unpack_weight(words, scales, fmt):
    g, p, n, _ = words.shape
    if fmt == "e4m3":
        vals = np.ascontiguousarray(words).view(ml_dtypes.float8_e4m3fn).astype(np.float64)
    else:
        nib = np.empty((g, p, n, 4), np.uint8)
        nib[..., 0::2] = words & 0xF
        nib[..., 1::2] = words >> 4
        vals = E2M1[nib]
    vals = vals * np.repeat(np.exp2(scales.astype(np.float64) - 127.0), 8, axis=1)[..., None]
    return vals.transpose(0, 1, 3, 2).reshape(g * 512, n)


B, N, P, C, HID, NB, E, MAXLEN = 2, 32, 3, 256, 128, 63, 1024, 2056
EPS = 1e-5
FMT = "e4m3"


def setup_inputs():
    s, t = mx_kscale(E), mx_kscale(E)
    h1 = bf(np.maximum(np.random.standard_normal((B, N, N, E)), 0.0) * s)
    edge_mask = bf(np.random.random((B, N, N)) > 0.15)
    W2_words, W2_scales = pack_weight(np.random.standard_normal((E, E)) * 1.4 / np.sqrt(E) / s[:, None] * t, FMT)
    b2 = bf(np.random.standard_normal(E) * 0.3 * t)
    W3_words, W3_scales = pack_weight(np.random.standard_normal((E, E)) * 1.4 / np.sqrt(E) / t[:, None], FMT)
    b3 = bf(np.random.standard_normal(E) * 0.3)
    ln_g = bf(1.0 + 0.2 * np.random.standard_normal(E))
    ln_b = bf(0.2 * np.random.standard_normal(E))
    return {"h1": h1,
            "edge_mask": edge_mask,
            "W2_words": W2_words,
            "W2_scales": W2_scales,
            "b2": b2,
            "W3_words": W3_words,
            "W3_scales": W3_scales,
            "b3": b3,
            "ln_g": ln_g,
            "ln_b": ln_b}


def reference(h1, edge_mask, W2_words, W2_scales, b2, W3_words, W3_scales, b3, ln_g, ln_b):
    h = np.maximum((mxq(f64(h1), 3, "e4m3") @ unpack_weight(W2_words, W2_scales, FMT)) + f64(b2), 0.0)
    h = (mxq(h, 3, "e4m3") @ unpack_weight(W3_words, W3_scales, FMT)) + f64(b3)
    mu = h.mean(-1, keepdims=True)
    var = h.var(-1, keepdims=True)
    h = (h - mu) / np.sqrt(var + EPS) * f64(ln_g) + f64(ln_b)
    return h * f64(edge_mask)[..., None]

@@ -1,0 +1,312 @@
+from contextlib import ExitStack
+
+import concourse.mybir as mybir
+from concourse.masks import make_identity
+
+F32 = mybir.dt.float32
+BF16 = mybir.dt.bfloat16
+I32 = mybir.dt.int32
+U32 = mybir.dt.uint32
+U8 = mybir.dt.uint8
+FP8X4 = mybir.dt.float8_e4m3fn_x4
+ALU = mybir.AluOpType
+ACT = mybir.ActivationFunctionType
+
+P = 128
+PACK = 4
+K_PASS = P * PACK
+FEATURES = 1024
+TOKENS = 2 * 32 * 32
+TILES = TOKENS // P
+PASSES = FEATURES // K_PASS
+BANK = 512
+HALVES = FEATURES // BANK
+EPS = 1e-5
+
+FLOPS = 2 * 2 * TOKENS * FEATURES * FEATURES
+
+
+def tile_edgefeaturenet_pb_kernel(
+    tc, h1, edge_mask, W2_words, W2_scales, b2, W3_words, W3_scales, b3, ln_g, ln_b, out
+):
+    nc = tc.nc
+    h1_rows = h1.rearrange("b n (h i) k -> (b n h) i k", i=TILES)
+    mask_rows = edge_mask.rearrange("b n (h i) -> (b n h) i", i=TILES)
+    out_rows = out.rearrange("b n (h i) k -> (b n h) i k", i=TILES)
+
+    with ExitStack() as stack:
+        stack.enter_context(tc.manual_schedule())
+        keep = stack.enter_context(tc.tile_pool(name="keep", bufs=1))
+        stage = stack.enter_context(tc.tile_pool(name="stage", bufs=3))
+        rows = stack.enter_context(tc.tile_pool(name="rows", bufs=3))
+        stats = stack.enter_context(tc.tile_pool(name="stats", bufs=4))
+        psum_x = stack.enter_context(tc.psum_pool(name="psum_x", bufs=1))
+        psum_h = stack.enter_context(tc.psum_pool(name="psum_h", bufs=1))
+        psum_acc = stack.enter_context(tc.psum_pool(name="psum_acc", bufs=6))
+
+        h1_sb = keep.tile([P, TILES, FEATURES], BF16, name="h1_sb")
+        w2_words = keep.tile([P, PASSES, FEATURES], U32, align_bytes=64, name="w2_words")
+        w3_words = keep.tile([P, PASSES, FEATURES], U32, align_bytes=64, name="w3_words")
+        planes = keep.tile([P, FEATURES], U8, align_bytes=64, name="planes")
+        nc.vector.memset(planes[:].bitcast(I32), 0)
+        vec_rows = keep.tile([P, FEATURES], BF16, name="vec_rows")
+        nc.vector.memset(vec_rows[:], 0.0)
+        mask_bf16 = keep.tile([P, TILES], BF16, name="mask_bf16")
+
+        def load_tokens(first_tile, end_tile):
+            nc.sync.dma_start(out=h1_sb[:, first_tile:end_tile, :], in_=h1_rows[:, first_tile:end_tile, :])
+
+        def load_scales(scales, first_plane):
+            for quadrant in range(4):
+                first = 32 * quadrant + 4 * first_plane
+                nc.sync.dma_start(
+                    out=planes[first : first + 4 * PASSES, :].bitcast(I32),
+                    in_=scales[:, 4 * quadrant : 4 * quadrant + 4, :].bitcast(I32),
+                )
+
+        def load_words(words_sb, words):
+            by_partition = words.rearrange("g p n t -> p g (n t)")
+            for n in range(HALVES):
+                nc.sync.dma_start(
+                    out=words_sb[:, :, n * BANK : (n + 1) * BANK].bitcast(I32),
+                    in_=by_partition[:, :, n * BANK * PACK : (n + 1) * BANK * PACK].bitcast(I32),
+                )
+
+        def load_vector(v, vec):
+            nc.sync.dma_start(out=vec_rows[32 * v : 32 * v + 1, :], in_=vec.rearrange("(o n) -> o n", o=1))
+
+        load_tokens(0, 1)
+        load_scales(W2_scales, 0)
+        load_vector(0, b2)
+        load_words(w2_words, W2_words)
+        load_vector(1, b3)
+        load_vector(2, ln_g)
+        load_vector(3, ln_b)
+        nc.sync.dma_start(out=mask_bf16[:], in_=mask_rows)
+        load_tokens(1, 2)
+        load_scales(W3_scales, PASSES)
+        load_words(w3_words, W3_words)
+        load_tokens(2, 4)
+        load_tokens(4, 8)
+        load_tokens(8, TILES)
+
+        ident_f32 = keep.tile([P, P], F32, name="ident_f32")
+        make_identity(nc, ident_f32[:])
+        ident_bf16 = keep.tile([P, P], BF16, name="ident_bf16")
+        make_identity(nc, ident_bf16[:])
+        eps = keep.tile([P, 1], F32, name="eps")
+        nc.vector.memset(eps[:], EPS)
+        warm = keep.tile([P, 1], F32, name="warm")
+        nc.scalar.activation(out=warm[:], in_=eps[:], func=ACT.Sqrt)
+
+        b2_sorted = keep.tile([P, PASSES, PACK, P], BF16, name="b2_sorted")
+        b3_all = keep.tile([P, FEATURES], BF16, name="b3_all")
+        gain_all = keep.tile([P, FEATURES], BF16, name="gain_all")
+        shift_all = keep.tile([P, FEATURES], BF16, name="shift_all")
+        mask = keep.tile([P, TILES], F32, name="mask")
+
+        def spread_vector(v, spread):
+            for n in range(HALVES):
+                cols = slice(n * BANK, (n + 1) * BANK)
+                acc = psum_acc.tile([P, BANK], F32, name="acc")
+                nc.tensor.matmul(
+                    out=acc[:],
+                    lhsT=ident_bf16[:, 32 * v : 32 * v + 1].to_broadcast([P, P]),
+                    rhs=vec_rows[:, cols],
+                    start=True,
+                    stop=True,
+                )
+                if spread is b2_sorted:
+                    nc.vector.tensor_copy(
+                        out=b2_sorted[:, n, :, :], in_=acc[:].rearrange("p (c t) -> p t c", t=PACK)
+                    )
+                else:
+                    nc.scalar.copy(out=spread[:, cols], in_=acc[:])
+
+        xt, x_grouped, x_mx, h_banks, h_rows, ht, h_grouped, h_mx = {}, {}, {}, {}, {}, {}, {}, {}
+        y_banks, y, neg_mean, std, slope, offset, norm, gained = {}, {}, {}, {}, {}, {}, {}, {}
+
+        def transpose_tokens(i):
+            pairs = h1_sb[:, i, :].bitcast(F32)
+            xt[i] = psum_x.tile([P, PASSES, 2, P], F32, name="xt")
+            for g in range(PASSES):
+                for u in range(2):
+                    nc.tensor.transpose(
+                        xt[i][:, g, u, :], pairs[:, 256 * g + u : 256 * (g + 1) : 2], ident_f32[:]
+                    )
+
+        def group_tokens(i):
+            x_grouped[i] = stage.tile([P, PASSES, P, PACK], BF16, align_bytes=64, name="x_grouped")
+            nc.scalar.copy(out=x_grouped[i][:].bitcast(F32), in_=xt[i][:].rearrange("p g u r -> p g r u"))
+
+        def quantise(grouped, tag):
+            codes = stage.tile([P, PASSES * P], U32, align_bytes=64, name="codes" + tag)
+            scales = stage.tile([P, PASSES * P], U8, align_bytes=64, name="scales" + tag)
+            nc.vector.quantize_mx(
+                out=codes[:].bitcast(FP8X4),
+                scales=scales[:],
+                in_=grouped[:].rearrange("p g r t -> p (g r t)"),
+            )
+            return codes, scales
+
+        def multiply(operand, words_sb, first_plane):
+            codes, scales = operand
+            banks = []
+            for n in range(HALVES):
+                cols = slice(n * BANK, (n + 1) * BANK)
+                acc = psum_acc.tile([P, BANK], F32, name="acc")
+                for g in range(PASSES):
+                    tokens = slice(g * P, (g + 1) * P)
+                    nc.tensor.matmul_mx(
+                        out=acc[:],
+                        lhsT=codes[:, tokens].bitcast(FP8X4),
+                        lhsT_scale=scales[:, tokens],
+                        rhs=words_sb[:, g, cols].bitcast(FP8X4),
+                        rhs_scale=planes[4 * (first_plane + g) : P, cols],
+                        start=(g == 0),
+                        stop=(g == PASSES - 1),
+                    )
+                banks.append(acc)
+            return banks
+
+        def add_bias(i):
+            h_rows[i] = stage.tile([P, PASSES, PACK, P], BF16, name="h_rows")
+            for g in range(PASSES):
+                nc.vector.tensor_tensor(
+                    out=h_rows[i][:, g, :, :],
+                    in0=h_banks[i][g][:].rearrange("p (c t) -> p t c", t=PACK),
+                    in1=b2_sorted[:, g, :, :],
+                    op=ALU.add,
+                )
+
+        def transpose_hidden(i):
+            ht[i] = psum_h.tile([P, PASSES, PACK, P], BF16, name="ht")
+            for g in range(PASSES):
+                for t in range(PACK):
+                    nc.tensor.transpose(ht[i][:, g, t, :], h_rows[i][:, g, t, :], ident_bf16[:])
+
+        def group_hidden(i):
+            h_grouped[i] = stage.tile([P, PASSES, P, PACK], BF16, align_bytes=64, name="h_grouped")
+            nc.scalar.activation(
+                out=h_grouped[i][:], in_=ht[i][:].rearrange("p g t r -> p g r t"), func=ACT.Relu
+            )
+
+        def add_bias_and_sum(i):
+            y[i] = rows.tile([P, FEATURES], F32, name="y")
+            sums = stats.tile([P, HALVES], F32, name="sums")
+            for n in range(HALVES):
+                cols = slice(n * BANK, (n + 1) * BANK)
+                nc.vector.scalar_tensor_tensor(
+                    out=y[i][:, cols],
+                    in0=y_banks[i][n][:],
+                    scalar=1.0,
+                    in1=b3_all[:, cols],
+                    op0=ALU.mult,
+                    op1=ALU.add,
+                    accum_out=sums[:, n : n + 1],
+                )
+            neg_mean[i] = stats.tile([P, 1], F32, name="neg_mean")
+            nc.vector.tensor_scalar(
+                out=neg_mean[i][:],
+                in0=sums[:, 0:1],
+                scalar1=sums[:, 1:2],
+                scalar2=-1.0 / FEATURES,
+                op0=ALU.add,
+                op1=ALU.mult,
+            )
+
+        def deviation(i):
+            squares = rows.tile([P, FEATURES], BF16, name="squares")
+            sum_sq = stats.tile([P, 1], F32, name="sum_sq")
+            nc.scalar.activation(
+                out=squares[:],
+                in_=y[i][:],
+                func=ACT.Square,
+                bias=neg_mean[i][:, 0:1],
+                scale=1.0,
+                accum_out=sum_sq[:],
+            )
+            std[i] = stats.tile([P, 1], F32, name="std")
+            nc.scalar.activation(
+                out=std[i][:], in_=sum_sq[:], func=ACT.Sqrt, bias=eps[:, 0:1], scale=1.0 / FEATURES
+            )
+
+        def slope_and_offset(i):
+            rstd = stats.tile([P, 1], F32, name="rstd")
+            nc.vector.reciprocal(out=rstd[:], in_=std[i][:])
+            slope[i] = stats.tile([P, 1], F32, name="slope")
+            nc.vector.tensor_scalar(
+                out=slope[i][:], in0=rstd[:], scalar1=mask[:, i : i + 1], scalar2=None, op0=ALU.mult
+            )
+            offset[i] = stats.tile([P, 1], F32, name="offset")
+            nc.vector.tensor_scalar(
+                out=offset[i][:], in0=slope[i][:], scalar1=neg_mean[i][:, 0:1], scalar2=None, op0=ALU.mult
+            )
+
+        def normalise(i):
+            norm[i] = rows.tile([P, FEATURES], F32, name="norm")
+            nc.scalar.activation(
+                out=norm[i][:], in_=y[i][:], func=ACT.Identity, bias=offset[i][:, 0:1], scale=slope[i][:, 0:1]
+            )
+
+        def gain(i):
+            gained[i] = rows.tile([P, FEATURES], F32, name="gained")
+            nc.gpsimd.tensor_tensor(out=gained[i][:], in0=norm[i][:], in1=gain_all[:], op=ALU.mult)
+
+        def shift_and_store(i):
+            result = rows.tile([P, FEATURES], F32, name="result")
+            nc.vector.scalar_tensor_tensor(
+                out=result[:],
+                in0=shift_all[:],
+                scalar=mask[:, i : i + 1],
+                in1=gained[i][:],
+                op0=ALU.mult,
+                op1=ALU.add,
+            )
+            nc.sync.dma_start(out=out_rows[:, i, :], in_=result[:])
+
+        def tile_exists(i):
+            return 0 <= i < TILES
+
+        def work_of_round(r):
+            if tile_exists(r + 1):
+                transpose_tokens(r + 1)
+            if tile_exists(r - 1):
+                transpose_hidden(r - 1)
+            if tile_exists(r - 2):
+                y_banks[r - 2] = multiply(h_mx[r - 2], w3_words, PASSES)
+            if tile_exists(r):
+                h_banks[r] = multiply(x_mx[r], w2_words, 0)
+            if tile_exists(r - 3):
+                slope_and_offset(r - 3)
+            if tile_exists(r + 1):
+                group_tokens(r + 1)
+                x_mx[r + 1] = quantise(x_grouped[r + 1], "_x")
+            if tile_exists(r - 2):
+                add_bias_and_sum(r - 2)
+            if tile_exists(r - 1):
+                group_hidden(r - 1)
+            if tile_exists(r):
+                add_bias(r)
+            if tile_exists(r - 1):
+                h_mx[r - 1] = quantise(h_grouped[r - 1], "_h")
+            if tile_exists(r - 3):
+                normalise(r - 3)
+            if tile_exists(r - 2):
+                deviation(r - 2)
+            if tile_exists(r - 4):
+                gain(r - 4)
+            if tile_exists(r - 5):
+                shift_and_store(r - 5)
+
+        transpose_tokens(0)
+        group_tokens(0)
+        x_mx[0] = quantise(x_grouped[0], "_x")
+        spread_vector(0, b2_sorted)
+        work_of_round(0)
+        spread_vector(1, b3_all)
+        spread_vector(2, gain_all)
+        spread_vector(3, shift_all)
+        nc.vector.tensor_copy(out=mask[:], in_=mask_bf16[:])
+        for r in range(1, TILES + 5):
+            work_of_round(r)

@@ -40,6 +40,7 @@ def tile_edgefeaturenet_pb_kernel(
         stage = stack.enter_context(tc.tile_pool(name="stage", bufs=3))
         rows = stack.enter_context(tc.tile_pool(name="rows", bufs=3))
         stats = stack.enter_context(tc.tile_pool(name="stats", bufs=4))
+        handover = stack.enter_context(tc.tile_pool(name="handover", bufs=1))
         psum_x = stack.enter_context(tc.psum_pool(name="psum_x", bufs=1))
         psum_h = stack.enter_context(tc.psum_pool(name="psum_h", bufs=1))
         psum_acc = stack.enter_context(tc.psum_pool(name="psum_acc", bufs=6))
@@ -97,7 +98,7 @@ def tile_edgefeaturenet_pb_kernel(
         eps = keep.tile([P, 1], F32, name="eps")
         nc.vector.memset(eps[:], EPS)
         warm = keep.tile([P, 1], F32, name="warm")
-        nc.scalar.activation(out=warm[:], in_=eps[:], func=ACT.Sqrt)
+        nc.scalar.activation(out=warm[:], in_=eps[:], func=ACT.Abs_reciprocal_sqrt)
 
         b2_sorted = keep.tile([P, PASSES, PACK, P], BF16, name="b2_sorted")
         b3_all = keep.tile([P, FEATURES], BF16, name="b3_all")
@@ -124,7 +125,8 @@ def tile_edgefeaturenet_pb_kernel(
                     nc.scalar.copy(out=spread[:, cols], in_=acc[:])
 
         xt, x_grouped, x_mx, h_banks, h_rows, ht, h_grouped, h_mx = {}, {}, {}, {}, {}, {}, {}, {}
-        y_banks, y, neg_mean, std, slope, offset, norm, gained = {}, {}, {}, {}, {}, {}, {}, {}
+        y_banks, y, sums, neg_mean, masked_neg_mean, sum_sq, rstd = {}, {}, {}, {}, {}, {}, {}
+        slope, offset, norm, gained = {}, {}, {}, {}
 
         def transpose_tokens(i):
             pairs = h1_sb[:, i, :].bitcast(F32)
@@ -169,15 +171,15 @@ def tile_edgefeaturenet_pb_kernel(
                 banks.append(acc)
             return banks
 
-        def add_bias(i):
-            h_rows[i] = stage.tile([P, PASSES, PACK, P], BF16, name="h_rows")
-            for g in range(PASSES):
-                nc.vector.tensor_tensor(
-                    out=h_rows[i][:, g, :, :],
-                    in0=h_banks[i][g][:].rearrange("p (c t) -> p t c", t=PACK),
-                    in1=b2_sorted[:, g, :, :],
-                    op=ALU.add,
-                )
+        def add_bias(i, g):
+            if g == 0:
+                h_rows[i] = stage.tile([P, PASSES, PACK, P], BF16, name="h_rows")
+            nc.vector.tensor_tensor(
+                out=h_rows[i][:, g, :, :],
+                in0=h_banks[i][g][:].rearrange("p (c t) -> p t c", t=PACK),
+                in1=b2_sorted[:, g, :, :],
+                op=ALU.add,
+            )
 
         def transpose_hidden(i):
             ht[i] = psum_h.tile([P, PASSES, PACK, P], BF16, name="ht")
@@ -193,7 +195,7 @@ def tile_edgefeaturenet_pb_kernel(
 
         def add_bias_and_sum(i):
             y[i] = rows.tile([P, FEATURES], F32, name="y")
-            sums = stats.tile([P, HALVES], F32, name="sums")
+            sums[i] = stats.tile([P, HALVES], F32, name="sums")
             for n in range(HALVES):
                 cols = slice(n * BANK, (n + 1) * BANK)
                 nc.vector.scalar_tensor_tensor(
@@ -203,44 +205,56 @@ def tile_edgefeaturenet_pb_kernel(
                     in1=b3_all[:, cols],
                     op0=ALU.mult,
                     op1=ALU.add,
-                    accum_out=sums[:, n : n + 1],
+                    accum_out=sums[i][:, n : n + 1],
                 )
+
+        def mean(i):
             neg_mean[i] = stats.tile([P, 1], F32, name="neg_mean")
             nc.vector.tensor_scalar(
                 out=neg_mean[i][:],
-                in0=sums[:, 0:1],
-                scalar1=sums[:, 1:2],
+                in0=sums[i][:, 0:1],
+                scalar1=sums[i][:, 1:2],
                 scalar2=-1.0 / FEATURES,
                 op0=ALU.add,
                 op1=ALU.mult,
             )
 
-        def deviation(i):
+        def mask_mean(i):
+            masked_neg_mean[i] = stats.tile([P, 1], F32, name="masked_neg_mean")
+            nc.vector.tensor_scalar(
+                out=masked_neg_mean[i][:], in0=neg_mean[i][:], scalar1=mask[:, i : i + 1], scalar2=None, op0=ALU.mult
+            )
+
+        def sum_squares(i):
             squares = rows.tile([P, FEATURES], BF16, name="squares")
-            sum_sq = stats.tile([P, 1], F32, name="sum_sq")
+            sum_sq[i] = stats.tile([P, 1], F32, name="sum_sq")
             nc.scalar.activation(
                 out=squares[:],
                 in_=y[i][:],
                 func=ACT.Square,
                 bias=neg_mean[i][:, 0:1],
                 scale=1.0,
-                accum_out=sum_sq[:],
+                accum_out=sum_sq[i][:],
             )
-            std[i] = stats.tile([P, 1], F32, name="std")
+
+        def inverse_deviation(i):
+            rstd[i] = stats.tile([P, 1], F32, name="rstd")
             nc.scalar.activation(
-                out=std[i][:], in_=sum_sq[:], func=ACT.Sqrt, bias=eps[:, 0:1], scale=1.0 / FEATURES
+                out=rstd[i][:],
+                in_=sum_sq[i][:],
+                func=ACT.Abs_reciprocal_sqrt,
+                bias=eps[:, 0:1],
+                scale=1.0 / FEATURES,
             )
 
         def slope_and_offset(i):
-            rstd = stats.tile([P, 1], F32, name="rstd")
-            nc.vector.reciprocal(out=rstd[:], in_=std[i][:])
             slope[i] = stats.tile([P, 1], F32, name="slope")
             nc.vector.tensor_scalar(
-                out=slope[i][:], in0=rstd[:], scalar1=mask[:, i : i + 1], scalar2=None, op0=ALU.mult
+                out=slope[i][:], in0=rstd[i][:], scalar1=mask[:, i : i + 1], scalar2=None, op0=ALU.mult
             )
             offset[i] = stats.tile([P, 1], F32, name="offset")
             nc.vector.tensor_scalar(
-                out=offset[i][:], in0=slope[i][:], scalar1=neg_mean[i][:, 0:1], scalar2=None, op0=ALU.mult
+                out=offset[i][:], in0=rstd[i][:], scalar1=masked_neg_mean[i][:, 0:1], scalar2=None, op0=ALU.mult
             )
 
         def normalise(i):
@@ -250,8 +264,12 @@ def tile_edgefeaturenet_pb_kernel(
             )
 
         def gain(i):
-            gained[i] = rows.tile([P, FEATURES], F32, name="gained")
-            nc.gpsimd.tensor_tensor(out=gained[i][:], in0=norm[i][:], in1=gain_all[:], op=ALU.mult)
+            gained[i] = handover.tile([P, FEATURES], F32, name="gained")
+            for n in range(HALVES):
+                cols = slice(n * BANK, (n + 1) * BANK)
+                nc.gpsimd.tensor_tensor(
+                    out=gained[i][:, cols], in0=norm[i][:, cols], in1=gain_all[:, cols], op=ALU.mult
+                )
 
         def shift_and_store(i):
             result = rows.tile([P, FEATURES], F32, name="result")
@@ -269,35 +287,40 @@ def tile_edgefeaturenet_pb_kernel(
             return 0 <= i < TILES
 
         def work_of_round(r):
-            if tile_exists(r + 1):
-                transpose_tokens(r + 1)
-            if tile_exists(r - 1):
-                transpose_hidden(r - 1)
+            if tile_exists(r - 4):
+                normalise(r - 4)
+            if tile_exists(r - 5):
+                shift_and_store(r - 5)
+            if tile_exists(r - 4):
+                gain(r - 4)
             if tile_exists(r - 2):
                 y_banks[r - 2] = multiply(h_mx[r - 2], w3_words, PASSES)
+                add_bias_and_sum(r - 2)
             if tile_exists(r):
                 h_banks[r] = multiply(x_mx[r], w2_words, 0)
-            if tile_exists(r - 3):
-                slope_and_offset(r - 3)
-            if tile_exists(r + 1):
-                group_tokens(r + 1)
-                x_mx[r + 1] = quantise(x_grouped[r + 1], "_x")
-            if tile_exists(r - 2):
-                add_bias_and_sum(r - 2)
             if tile_exists(r - 1):
                 group_hidden(r - 1)
             if tile_exists(r):
-                add_bias(r)
+                add_bias(r, 0)
+                add_bias(r, 1)
+            if tile_exists(r - 2):
+                mean(r - 2)
+            if tile_exists(r - 3):
+                sum_squares(r - 3)
+            if tile_exists(r + 1):
+                transpose_tokens(r + 1)
+            if tile_exists(r):
+                transpose_hidden(r)
             if tile_exists(r - 1):
                 h_mx[r - 1] = quantise(h_grouped[r - 1], "_h")
-            if tile_exists(r - 3):
-                normalise(r - 3)
             if tile_exists(r - 2):
-                deviation(r - 2)
-            if tile_exists(r - 4):
-                gain(r - 4)
-            if tile_exists(r - 5):
-                shift_and_store(r - 5)
+                mask_mean(r - 2)
+            if tile_exists(r + 1):
+                group_tokens(r + 1)
+                x_mx[r + 1] = quantise(x_grouped[r + 1], "_x")
+            if tile_exists(r - 3):
+                inverse_deviation(r - 3)
+                slope_and_offset(r - 3)
 
         transpose_tokens(0)
         group_tokens(0)

@@ -38,7 +38,7 @@ def tile_edgefeaturenet_pb_kernel(
         stack.enter_context(tc.manual_schedule())
         keep = stack.enter_context(tc.tile_pool(name="keep", bufs=1))
         stage = stack.enter_context(tc.tile_pool(name="stage", bufs=3))
-        rows = stack.enter_context(tc.tile_pool(name="rows", bufs=3))
+        rows = stack.enter_context(tc.tile_pool(name="rows", bufs=4))
         stats = stack.enter_context(tc.tile_pool(name="stats", bufs=4))
         handover = stack.enter_context(tc.tile_pool(name="handover", bufs=1))
         psum_x = stack.enter_context(tc.psum_pool(name="psum_x", bufs=1))
@@ -76,7 +76,7 @@ def tile_edgefeaturenet_pb_kernel(
         def load_vector(v, vec):
             nc.sync.dma_start(out=vec_rows[32 * v : 32 * v + 1, :], in_=vec.rearrange("(o n) -> o n", o=1))
 
-        load_tokens(0, 1)
+        load_tokens(0, 2)
         load_scales(W2_scales, 0)
         load_vector(0, b2)
         load_words(w2_words, W2_words)
@@ -84,10 +84,9 @@ def tile_edgefeaturenet_pb_kernel(
         load_vector(2, ln_g)
         load_vector(3, ln_b)
         nc.sync.dma_start(out=mask_bf16[:], in_=mask_rows)
-        load_tokens(1, 2)
+        load_tokens(2, 4)
         load_scales(W3_scales, PASSES)
         load_words(w3_words, W3_words)
-        load_tokens(2, 4)
         load_tokens(4, 8)
         load_tokens(8, TILES)
 
@@ -259,9 +258,15 @@ def tile_edgefeaturenet_pb_kernel(
 
         def normalise(i):
             norm[i] = rows.tile([P, FEATURES], F32, name="norm")
-            nc.scalar.activation(
-                out=norm[i][:], in_=y[i][:], func=ACT.Identity, bias=offset[i][:, 0:1], scale=slope[i][:, 0:1]
-            )
+            for n in range(HALVES):
+                cols = slice(n * BANK, (n + 1) * BANK)
+                nc.scalar.activation(
+                    out=norm[i][:, cols],
+                    in_=y[i][:, cols],
+                    func=ACT.Identity,
+                    bias=offset[i][:, 0:1],
+                    scale=slope[i][:, 0:1],
+                )
 
         def gain(i):
             gained[i] = handover.tile([P, FEATURES], F32, name="gained")
@@ -273,54 +278,58 @@ def tile_edgefeaturenet_pb_kernel(
 
         def shift_and_store(i):
             result = rows.tile([P, FEATURES], F32, name="result")
-            nc.vector.scalar_tensor_tensor(
-                out=result[:],
-                in0=shift_all[:],
-                scalar=mask[:, i : i + 1],
-                in1=gained[i][:],
-                op0=ALU.mult,
-                op1=ALU.add,
-            )
+            for n in range(HALVES):
+                cols = slice(n * BANK, (n + 1) * BANK)
+                nc.vector.scalar_tensor_tensor(
+                    out=result[:, cols],
+                    in0=shift_all[:, cols],
+                    scalar=mask[:, i : i + 1],
+                    in1=gained[i][:, cols],
+                    op0=ALU.mult,
+                    op1=ALU.add,
+                )
             nc.sync.dma_start(out=out_rows[:, i, :], in_=result[:])
 
         def tile_exists(i):
             return 0 <= i < TILES
 
         def work_of_round(r):
-            if tile_exists(r - 4):
-                normalise(r - 4)
-            if tile_exists(r - 5):
-                shift_and_store(r - 5)
-            if tile_exists(r - 4):
-                gain(r - 4)
+            if tile_exists(r - 6):
+                shift_and_store(r - 6)
             if tile_exists(r - 2):
-                y_banks[r - 2] = multiply(h_mx[r - 2], w3_words, PASSES)
-                add_bias_and_sum(r - 2)
+                group_hidden(r - 2)
+                h_mx[r - 2] = quantise(h_grouped[r - 2], "_h")
+            if tile_exists(r - 3):
+                y_banks[r - 3] = multiply(h_mx[r - 3], w3_words, PASSES)
+            if tile_exists(r - 5):
+                normalise(r - 5)
+            if tile_exists(r - 4):
+                sum_squares(r - 4)
+            if tile_exists(r + 1):
+                transpose_tokens(r + 1)
+            if tile_exists(r - 4):
+                mask_mean(r - 4)
+            if tile_exists(r - 1):
+                transpose_hidden(r - 1)
+            if tile_exists(r - 3):
+                add_bias_and_sum(r - 3)
             if tile_exists(r):
                 h_banks[r] = multiply(x_mx[r], w2_words, 0)
-            if tile_exists(r - 1):
-                group_hidden(r - 1)
+            if tile_exists(r + 1):
+                group_tokens(r + 1)
             if tile_exists(r):
                 add_bias(r, 0)
                 add_bias(r, 1)
-            if tile_exists(r - 2):
-                mean(r - 2)
+            if tile_exists(r - 4):
+                inverse_deviation(r - 4)
+            if tile_exists(r - 5):
+                gain(r - 5)
+            if tile_exists(r - 4):
+                slope_and_offset(r - 4)
             if tile_exists(r - 3):
-                sum_squares(r - 3)
+                mean(r - 3)
             if tile_exists(r + 1):
-                transpose_tokens(r + 1)
-            if tile_exists(r):
-                transpose_hidden(r)
-            if tile_exists(r - 1):
-                h_mx[r - 1] = quantise(h_grouped[r - 1], "_h")
-            if tile_exists(r - 2):
-                mask_mean(r - 2)
-            if tile_exists(r + 1):
-                group_tokens(r + 1)
                 x_mx[r + 1] = quantise(x_grouped[r + 1], "_x")
-            if tile_exists(r - 3):
-                inverse_deviation(r - 3)
-                slope_and_offset(r - 3)
 
         transpose_tokens(0)
         group_tokens(0)
@@ -331,5 +340,5 @@ def tile_edgefeaturenet_pb_kernel(
         spread_vector(2, gain_all)
         spread_vector(3, shift_all)
         nc.vector.tensor_copy(out=mask[:], in_=mask_bf16[:])
-        for r in range(1, TILES + 5):
+        for r in range(1, TILES + 6):
             work_of_round(r)

@@ -258,36 +258,24 @@ def tile_edgefeaturenet_pb_kernel(
 
         def normalise(i):
             norm[i] = rows.tile([P, FEATURES], F32, name="norm")
-            for n in range(HALVES):
-                cols = slice(n * BANK, (n + 1) * BANK)
-                nc.scalar.activation(
-                    out=norm[i][:, cols],
-                    in_=y[i][:, cols],
-                    func=ACT.Identity,
-                    bias=offset[i][:, 0:1],
-                    scale=slope[i][:, 0:1],
-                )
+            nc.scalar.activation(
+                out=norm[i][:], in_=y[i][:], func=ACT.Identity, bias=offset[i][:, 0:1], scale=slope[i][:, 0:1]
+            )
 
         def gain(i):
             gained[i] = handover.tile([P, FEATURES], F32, name="gained")
-            for n in range(HALVES):
-                cols = slice(n * BANK, (n + 1) * BANK)
-                nc.gpsimd.tensor_tensor(
-                    out=gained[i][:, cols], in0=norm[i][:, cols], in1=gain_all[:, cols], op=ALU.mult
-                )
+            nc.gpsimd.tensor_tensor(out=gained[i][:], in0=norm[i][:], in1=gain_all[:], op=ALU.mult)
 
         def shift_and_store(i):
             result = rows.tile([P, FEATURES], F32, name="result")
-            for n in range(HALVES):
-                cols = slice(n * BANK, (n + 1) * BANK)
-                nc.vector.scalar_tensor_tensor(
-                    out=result[:, cols],
-                    in0=shift_all[:, cols],
-                    scalar=mask[:, i : i + 1],
-                    in1=gained[i][:, cols],
-                    op0=ALU.mult,
-                    op1=ALU.add,
-                )
+            nc.vector.scalar_tensor_tensor(
+                out=result[:],
+                in0=shift_all[:],
+                scalar=mask[:, i : i + 1],
+                in1=gained[i][:],
+                op0=ALU.mult,
+                op1=ALU.add,
+            )
             nc.sync.dma_start(out=out_rows[:, i, :], in_=result[:])
 
         def tile_exists(i):

@@ -22,6 +22,7 @@ PASSES = FEATURES // K_PASS
 BANK = 512
 HALVES = FEATURES // BANK
 EPS = 1e-5
+GAINS_ON_VECTOR = 3
 
 FLOPS = 2 * 2 * TOKENS * FEATURES * FEATURES
 
@@ -76,7 +77,8 @@ def tile_edgefeaturenet_pb_kernel(
         def load_vector(v, vec):
             nc.sync.dma_start(out=vec_rows[32 * v : 32 * v + 1, :], in_=vec.rearrange("(o n) -> o n", o=1))
 
-        load_tokens(0, 2)
+        load_tokens(0, 1)
+        load_tokens(1, 2)
         load_scales(W2_scales, 0)
         load_vector(0, b2)
         load_words(w2_words, W2_words)
@@ -124,7 +126,7 @@ def tile_edgefeaturenet_pb_kernel(
                     nc.scalar.copy(out=spread[:, cols], in_=acc[:])
 
         xt, x_grouped, x_mx, h_banks, h_rows, ht, h_grouped, h_mx = {}, {}, {}, {}, {}, {}, {}, {}
-        y_banks, y, sums, neg_mean, masked_neg_mean, sum_sq, rstd = {}, {}, {}, {}, {}, {}, {}
+        y_banks, y, sums, neg_mean, sum_sq, rstd = {}, {}, {}, {}, {}, {}
         slope, offset, norm, gained = {}, {}, {}, {}
 
         def transpose_tokens(i):
@@ -218,12 +220,6 @@ def tile_edgefeaturenet_pb_kernel(
                 op1=ALU.mult,
             )
 
-        def mask_mean(i):
-            masked_neg_mean[i] = stats.tile([P, 1], F32, name="masked_neg_mean")
-            nc.vector.tensor_scalar(
-                out=masked_neg_mean[i][:], in0=neg_mean[i][:], scalar1=mask[:, i : i + 1], scalar2=None, op0=ALU.mult
-            )
-
         def sum_squares(i):
             squares = rows.tile([P, FEATURES], BF16, name="squares")
             sum_sq[i] = stats.tile([P, 1], F32, name="sum_sq")
@@ -252,8 +248,13 @@ def tile_edgefeaturenet_pb_kernel(
                 out=slope[i][:], in0=rstd[i][:], scalar1=mask[:, i : i + 1], scalar2=None, op0=ALU.mult
             )
             offset[i] = stats.tile([P, 1], F32, name="offset")
-            nc.vector.tensor_scalar(
-                out=offset[i][:], in0=rstd[i][:], scalar1=masked_neg_mean[i][:, 0:1], scalar2=None, op0=ALU.mult
+            nc.vector.scalar_tensor_tensor(
+                out=offset[i][:],
+                in0=rstd[i][:],
+                scalar=mask[:, i : i + 1],
+                in1=neg_mean[i][:],
+                op0=ALU.mult,
+                op1=ALU.mult,
             )
 
         def normalise(i):
@@ -264,7 +265,8 @@ def tile_edgefeaturenet_pb_kernel(
 
         def gain(i):
             gained[i] = handover.tile([P, FEATURES], F32, name="gained")
-            nc.gpsimd.tensor_tensor(out=gained[i][:], in0=norm[i][:], in1=gain_all[:], op=ALU.mult)
+            engine = nc.gpsimd if i < TILES - GAINS_ON_VECTOR else nc.vector
+            engine.tensor_tensor(out=gained[i][:], in0=norm[i][:], in1=gain_all[:], op=ALU.mult)
 
         def shift_and_store(i):
             result = rows.tile([P, FEATURES], F32, name="result")
@@ -295,8 +297,6 @@ def tile_edgefeaturenet_pb_kernel(
                 sum_squares(r - 4)
             if tile_exists(r + 1):
                 transpose_tokens(r + 1)
-            if tile_exists(r - 4):
-                mask_mean(r - 4)
             if tile_exists(r - 1):
                 transpose_hidden(r - 1)
             if tile_exists(r - 3):
@@ -312,10 +312,10 @@ def tile_edgefeaturenet_pb_kernel(
                 inverse_deviation(r - 4)
             if tile_exists(r - 5):
                 gain(r - 5)
-            if tile_exists(r - 4):
-                slope_and_offset(r - 4)
             if tile_exists(r - 3):
                 mean(r - 3)
+            if tile_exists(r - 4):
+                slope_and_offset(r - 4)
             if tile_exists(r + 1):
                 x_mx[r + 1] = quantise(x_grouped[r + 1], "_x")
 

@@ -21,6 +21,10 @@ TILES = TOKENS // P
 PASSES = FEATURES // K_PASS
 BANK = 512
 HALVES = FEATURES // BANK
+PAIR = 2
+PAIR_TOKENS = PAIR * P
+PAIRS = TILES // PAIR
+UNITS = PAIRS * PASSES
 EPS = 1e-5
 GAINS_ON_VECTOR = 3
 
@@ -38,29 +42,32 @@ def tile_edgefeaturenet_pb_kernel(
     with ExitStack() as stack:
         stack.enter_context(tc.manual_schedule())
         keep = stack.enter_context(tc.tile_pool(name="keep", bufs=1))
-        stage = stack.enter_context(tc.tile_pool(name="stage", bufs=3))
+        stage = stack.enter_context(tc.tile_pool(name="stage", bufs=4))
         rows = stack.enter_context(tc.tile_pool(name="rows", bufs=4))
         stats = stack.enter_context(tc.tile_pool(name="stats", bufs=4))
-        handover = stack.enter_context(tc.tile_pool(name="handover", bufs=1))
-        psum_x = stack.enter_context(tc.psum_pool(name="psum_x", bufs=1))
-        psum_h = stack.enter_context(tc.psum_pool(name="psum_h", bufs=1))
-        psum_acc = stack.enter_context(tc.psum_pool(name="psum_acc", bufs=6))
+        handover = stack.enter_context(tc.tile_pool(name="handover", bufs=2))
+        psum_x = stack.enter_context(tc.psum_pool(name="psum_x", bufs=2))
+        psum_h = stack.enter_context(tc.psum_pool(name="psum_h", bufs=2))
+        psum_acc = stack.enter_context(tc.psum_pool(name="psum_acc", bufs=4))
 
         h1_sb = keep.tile([P, TILES, FEATURES], BF16, name="h1_sb")
         w2_words = keep.tile([P, PASSES, FEATURES], U32, align_bytes=64, name="w2_words")
         w3_words = keep.tile([P, PASSES, FEATURES], U32, align_bytes=64, name="w3_words")
-        planes = keep.tile([P, FEATURES], U8, align_bytes=64, name="planes")
-        nc.vector.memset(planes[:].bitcast(I32), 0)
+        w2_planes = keep.tile([P, FEATURES], U8, align_bytes=64, name="w2_planes")
+        nc.vector.memset(w2_planes[:].bitcast(I32), 0)
+        w3_planes = keep.tile([P, FEATURES], U8, align_bytes=64, name="w3_planes")
+        nc.vector.memset(w3_planes[:].bitcast(I32), 0)
         vec_rows = keep.tile([P, FEATURES], BF16, name="vec_rows")
         nc.vector.memset(vec_rows[:], 0.0)
         mask_bf16 = keep.tile([P, TILES], BF16, name="mask_bf16")
+        b2_bf16 = keep.tile([P, PASSES, PACK], BF16, name="b2_bf16")
 
         def load_tokens(first_tile, end_tile):
             nc.sync.dma_start(out=h1_sb[:, first_tile:end_tile, :], in_=h1_rows[:, first_tile:end_tile, :])
 
-        def load_scales(scales, first_plane):
+        def load_scales(planes, scales):
             for quadrant in range(4):
-                first = 32 * quadrant + 4 * first_plane
+                first = 32 * quadrant
                 nc.sync.dma_start(
                     out=planes[first : first + 4 * PASSES, :].bitcast(I32),
                     in_=scales[:, 4 * quadrant : 4 * quadrant + 4, :].bitcast(I32),
@@ -79,18 +86,19 @@ def tile_edgefeaturenet_pb_kernel(
 
         load_tokens(0, 1)
         load_tokens(1, 2)
-        load_scales(W2_scales, 0)
-        load_vector(0, b2)
+        load_scales(w2_planes, W2_scales)
+        nc.sync.dma_start(out=b2_bf16[:], in_=b2.rearrange("(a p t) -> p a t", a=PASSES, t=PACK))
         load_words(w2_words, W2_words)
+        load_tokens(2, 4)
         load_vector(1, b3)
         load_vector(2, ln_g)
         load_vector(3, ln_b)
         nc.sync.dma_start(out=mask_bf16[:], in_=mask_rows)
-        load_tokens(2, 4)
-        load_scales(W3_scales, PASSES)
+        load_scales(w3_planes, W3_scales)
+        load_tokens(4, 6)
         load_words(w3_words, W3_words)
-        load_tokens(4, 8)
-        load_tokens(8, TILES)
+        load_tokens(6, 10)
+        load_tokens(10, TILES)
 
         ident_f32 = keep.tile([P, P], F32, name="ident_f32")
         make_identity(nc, ident_f32[:])
@@ -101,11 +109,26 @@ def tile_edgefeaturenet_pb_kernel(
         warm = keep.tile([P, 1], F32, name="warm")
         nc.scalar.activation(out=warm[:], in_=eps[:], func=ACT.Abs_reciprocal_sqrt)
 
-        b2_sorted = keep.tile([P, PASSES, PACK, P], BF16, name="b2_sorted")
+        b2_cols = keep.tile([P, PASSES * PACK], F32, name="b2_cols")
         b3_all = keep.tile([P, FEATURES], BF16, name="b3_all")
         gain_all = keep.tile([P, FEATURES], BF16, name="gain_all")
         shift_all = keep.tile([P, FEATURES], BF16, name="shift_all")
         mask = keep.tile([P, TILES], F32, name="mask")
+
+        w2_sorted = keep.tile([P, PASSES, PASSES * PACK, P], U32, align_bytes=64, name="w2_sorted")
+        w2_planes_sorted = keep.tile([P, FEATURES], U8, align_bytes=64, name="w2_planes_sorted")
+
+        def sort_scales():
+            nc.vector.tensor_copy(
+                out=w2_planes_sorted[:].rearrange("p (a t m) -> p a m t", a=PASSES, t=PACK),
+                in_=w2_planes[:].rearrange("p (a m t) -> p a m t", a=PASSES, t=PACK),
+            )
+
+        def sort_words(a):
+            nc.vector.tensor_copy(
+                out=w2_sorted[:, :, PACK * a : PACK * (a + 1), :].bitcast(I32),
+                in_=w2_words[:, :, a * K_PASS : (a + 1) * K_PASS].bitcast(I32).rearrange("p g (m t) -> p g t m", t=PACK),
+            )
 
         def spread_vector(v, spread):
             for n in range(HALVES):
@@ -118,14 +141,12 @@ def tile_edgefeaturenet_pb_kernel(
                     start=True,
                     stop=True,
                 )
-                if spread is b2_sorted:
-                    nc.vector.tensor_copy(
-                        out=b2_sorted[:, n, :, :], in_=acc[:].rearrange("p (c t) -> p t c", t=PACK)
-                    )
+                if n == 0:
+                    nc.vector.tensor_copy(out=spread[:, cols], in_=acc[:])
                 else:
                     nc.scalar.copy(out=spread[:, cols], in_=acc[:])
 
-        xt, x_grouped, x_mx, h_banks, h_rows, ht, h_grouped, h_mx = {}, {}, {}, {}, {}, {}, {}, {}
+        xt, x_grouped, x_mx, h_banks, h_planes, h_grouped, h_mx = {}, {}, {}, {}, {}, {}, {}
         y_banks, y, sums, neg_mean, sum_sq, rstd = {}, {}, {}, {}, {}, {}
         slope, offset, norm, gained = {}, {}, {}, {}
 
@@ -139,60 +160,82 @@ def tile_edgefeaturenet_pb_kernel(
                     )
 
         def group_tokens(i):
-            x_grouped[i] = stage.tile([P, PASSES, P, PACK], BF16, align_bytes=64, name="x_grouped")
-            nc.scalar.copy(out=x_grouped[i][:].bitcast(F32), in_=xt[i][:].rearrange("p g u r -> p g r u"))
-
-        def quantise(grouped, tag):
-            codes = stage.tile([P, PASSES * P], U32, align_bytes=64, name="codes" + tag)
-            scales = stage.tile([P, PASSES * P], U8, align_bytes=64, name="scales" + tag)
-            nc.vector.quantize_mx(
-                out=codes[:].bitcast(FP8X4),
-                scales=scales[:],
-                in_=grouped[:].rearrange("p g r t -> p (g r t)"),
+            q, j = divmod(i, PAIR)
+            if j == 0:
+                x_grouped[q] = stage.tile([P, PASSES, PAIR_TOKENS, PACK], BF16, align_bytes=64, name="x_grouped")
+            nc.scalar.copy(
+                out=x_grouped[q][:, :, j * P : (j + 1) * P, :].bitcast(F32),
+                in_=xt[i][:].rearrange("p g u r -> p g r u"),
             )
+
+        def quantise(grouped_flat, width, tag):
+            codes = stage.tile([P, width], U32, align_bytes=64, name="codes" + tag)
+            scales = stage.tile([P, width], U8, align_bytes=64, name="scales" + tag)
+            nc.vector.quantize_mx(out=codes[:].bitcast(FP8X4), scales=scales[:], in_=grouped_flat)
             return codes, scales
 
-        def multiply(operand, words_sb, first_plane):
-            codes, scales = operand
-            banks = []
+        def quantise_tokens(q):
+            x_mx[q] = quantise(x_grouped[q][:].rearrange("p g r t -> p (g r t)"), PASSES * PAIR_TOKENS, "_x")
+
+        def multiply_first(unit):
+            q, a = divmod(unit, PASSES)
+            codes, scales = x_mx[q]
+            h_banks[unit] = []
+            for half in range(2):
+                bank = psum_h.tile([P, 2, PAIR_TOKENS], F32, name="hb")
+                for e in range(2):
+                    block = PACK * a + 2 * half + e
+                    for g in range(PASSES):
+                        tokens = slice(g * PAIR_TOKENS, (g + 1) * PAIR_TOKENS)
+                        nc.tensor.matmul_mx(
+                            out=bank[:, e, :],
+                            lhsT=w2_sorted[:, g, block, :].bitcast(FP8X4),
+                            lhsT_scale=w2_planes_sorted[4 * g : P, block * P : (block + 1) * P],
+                            rhs=codes[:, tokens].bitcast(FP8X4),
+                            rhs_scale=scales[:, tokens],
+                            start=(g == 0),
+                            stop=(g == PASSES - 1),
+                        )
+                h_banks[unit].append(bank)
+
+        def bias_and_relu(unit):
+            a = unit % PASSES
+            h_planes[unit] = stage.tile([P, PACK, PAIR_TOKENS], BF16, name="h_planes")
+            for t in range(PACK):
+                nc.scalar.activation(
+                    out=h_planes[unit][:, t, :],
+                    in_=h_banks[unit][t // 2][:, t % 2, :],
+                    func=ACT.Relu,
+                    bias=b2_cols[:, PACK * a + t : PACK * a + t + 1],
+                    scale=1.0,
+                )
+
+        def group_hidden(unit):
+            h_grouped[unit] = stage.tile([P, PAIR_TOKENS, PACK], BF16, align_bytes=64, name="h_grouped")
+            nc.vector.tensor_copy(out=h_grouped[unit][:], in_=h_planes[unit][:].rearrange("p t r -> p r t"))
+
+        def quantise_hidden(unit):
+            h_mx[unit] = quantise(h_grouped[unit][:].rearrange("p r t -> p (r t)"), PAIR_TOKENS, "_h")
+
+        def multiply_second(i):
+            q, j = divmod(i, PAIR)
+            tokens = slice(j * P, (j + 1) * P)
+            y_banks[i] = []
             for n in range(HALVES):
                 cols = slice(n * BANK, (n + 1) * BANK)
                 acc = psum_acc.tile([P, BANK], F32, name="acc")
-                for g in range(PASSES):
-                    tokens = slice(g * P, (g + 1) * P)
+                for a in range(PASSES):
+                    codes, scales = h_mx[PASSES * q + a]
                     nc.tensor.matmul_mx(
                         out=acc[:],
                         lhsT=codes[:, tokens].bitcast(FP8X4),
                         lhsT_scale=scales[:, tokens],
-                        rhs=words_sb[:, g, cols].bitcast(FP8X4),
-                        rhs_scale=planes[4 * (first_plane + g) : P, cols],
-                        start=(g == 0),
-                        stop=(g == PASSES - 1),
+                        rhs=w3_words[:, a, cols].bitcast(FP8X4),
+                        rhs_scale=w3_planes[4 * a : P, cols],
+                        start=(a == 0),
+                        stop=(a == PASSES - 1),
                     )
-                banks.append(acc)
-            return banks
-
-        def add_bias(i, g):
-            if g == 0:
-                h_rows[i] = stage.tile([P, PASSES, PACK, P], BF16, name="h_rows")
-            nc.vector.tensor_tensor(
-                out=h_rows[i][:, g, :, :],
-                in0=h_banks[i][g][:].rearrange("p (c t) -> p t c", t=PACK),
-                in1=b2_sorted[:, g, :, :],
-                op=ALU.add,
-            )
-
-        def transpose_hidden(i):
-            ht[i] = psum_h.tile([P, PASSES, PACK, P], BF16, name="ht")
-            for g in range(PASSES):
-                for t in range(PACK):
-                    nc.tensor.transpose(ht[i][:, g, t, :], h_rows[i][:, g, t, :], ident_bf16[:])
-
-        def group_hidden(i):
-            h_grouped[i] = stage.tile([P, PASSES, P, PACK], BF16, align_bytes=64, name="h_grouped")
-            nc.scalar.activation(
-                out=h_grouped[i][:], in_=ht[i][:].rearrange("p g t r -> p g r t"), func=ACT.Relu
-            )
+                y_banks[i].append(acc)
 
         def add_bias_and_sum(i):
             y[i] = rows.tile([P, FEATURES], F32, name="y")
@@ -283,50 +326,54 @@ def tile_edgefeaturenet_pb_kernel(
         def tile_exists(i):
             return 0 <= i < TILES
 
-        def work_of_round(r):
-            if tile_exists(r - 6):
-                shift_and_store(r - 6)
-            if tile_exists(r - 2):
-                group_hidden(r - 2)
-                h_mx[r - 2] = quantise(h_grouped[r - 2], "_h")
-            if tile_exists(r - 3):
-                y_banks[r - 3] = multiply(h_mx[r - 3], w3_words, PASSES)
-            if tile_exists(r - 5):
-                normalise(r - 5)
-            if tile_exists(r - 4):
-                sum_squares(r - 4)
-            if tile_exists(r + 1):
-                transpose_tokens(r + 1)
-            if tile_exists(r - 1):
-                transpose_hidden(r - 1)
-            if tile_exists(r - 3):
-                add_bias_and_sum(r - 3)
-            if tile_exists(r):
-                h_banks[r] = multiply(x_mx[r], w2_words, 0)
-            if tile_exists(r + 1):
-                group_tokens(r + 1)
-            if tile_exists(r):
-                add_bias(r, 0)
-                add_bias(r, 1)
-            if tile_exists(r - 4):
-                inverse_deviation(r - 4)
-            if tile_exists(r - 5):
-                gain(r - 5)
-            if tile_exists(r - 3):
-                mean(r - 3)
-            if tile_exists(r - 4):
-                slope_and_offset(r - 4)
-            if tile_exists(r + 1):
-                x_mx[r + 1] = quantise(x_grouped[r + 1], "_x")
+        def unit_exists(unit):
+            return 0 <= unit < UNITS
 
-        transpose_tokens(0)
-        group_tokens(0)
-        x_mx[0] = quantise(x_grouped[0], "_x")
-        spread_vector(0, b2_sorted)
-        work_of_round(0)
+        def work_of_slot(s):
+            if unit_exists(s + 2):
+                multiply_first(s + 2)
+            if tile_exists(s + 5):
+                transpose_tokens(s + 5)
+            if tile_exists(s - 2):
+                sum_squares(s - 2)
+                inverse_deviation(s - 2)
+            if tile_exists(s - 1):
+                add_bias_and_sum(s - 1)
+            if unit_exists(s + 1):
+                group_hidden(s + 1)
+            if unit_exists(s + 2):
+                bias_and_relu(s + 2)
+            if tile_exists(s - 2):
+                slope_and_offset(s - 2)
+            if unit_exists(s + 1):
+                quantise_hidden(s + 1)
+            if tile_exists(s):
+                multiply_second(s)
+            if tile_exists(s - 2):
+                normalise(s - 2)
+                gain(s - 2)
+            if tile_exists(s - 3):
+                shift_and_store(s - 3)
+            if tile_exists(s + 5):
+                group_tokens(s + 5)
+            if tile_exists(s - 1):
+                mean(s - 1)
+            if (s + 3) % PAIR == 0 and 0 <= (s + 3) // PAIR < PAIRS:
+                quantise_tokens((s + 3) // PAIR)
+
+        work_of_slot(-5)
+        work_of_slot(-4)
+        nc.vector.tensor_copy(out=b2_cols[:], in_=b2_bf16[:].rearrange("p a t -> p (a t)"))
+        sort_scales()
+        sort_words(0)
+        work_of_slot(-3)
+        sort_words(1)
+        work_of_slot(-2)
         spread_vector(1, b3_all)
-        spread_vector(2, gain_all)
-        spread_vector(3, shift_all)
         nc.vector.tensor_copy(out=mask[:], in_=mask_bf16[:])
-        for r in range(1, TILES + 6):
-            work_of_round(r)
+        work_of_slot(-1)
+        spread_vector(2, gain_all)
+        work_of_slot(0)
+        spread_vector(3, shift_all)
+        for s in range(1, TILES + 4):
+            work_of_slot(s)

@@ -26,7 +26,10 @@ PAIR_TOKENS = PAIR * P
 PAIRS = TILES // PAIR
 UNITS = PAIRS * PASSES
 EPS = 1e-5
-GAINS_ON_VECTOR = 3
+GAIN_ROWS = (0, 2, 3)
+SHIFT_ROW = 4
+BIAS_ROW = 32
+BORROWED = 9
 
 FLOPS = 2 * 2 * TOKENS * FEATURES * FEATURES
 
@@ -45,10 +48,12 @@ def tile_edgefeaturenet_pb_kernel(
         stage = stack.enter_context(tc.tile_pool(name="stage", bufs=4))
         rows = stack.enter_context(tc.tile_pool(name="rows", bufs=4))
         stats = stack.enter_context(tc.tile_pool(name="stats", bufs=4))
-        handover = stack.enter_context(tc.tile_pool(name="handover", bufs=2))
-        psum_x = stack.enter_context(tc.psum_pool(name="psum_x", bufs=2))
+        handover = stack.enter_context(tc.tile_pool(name="handover", bufs=3))
+        psum_x = stack.enter_context(tc.psum_pool(name="psum_x", bufs=1))
         psum_h = stack.enter_context(tc.psum_pool(name="psum_h", bufs=2))
-        psum_acc = stack.enter_context(tc.psum_pool(name="psum_acc", bufs=4))
+        psum_acc = stack.enter_context(tc.psum_pool(name="psum_acc", bufs=2))
+        psum_rank = stack.enter_context(tc.psum_pool(name="psum_rank", bufs=2))
+        psum_coef = stack.enter_context(tc.psum_pool(name="psum_coef", bufs=1))
 
         h1_sb = keep.tile([P, TILES, FEATURES], BF16, name="h1_sb")
         w2_words = keep.tile([P, PASSES, FEATURES], U32, align_bytes=64, name="w2_words")
@@ -81,8 +86,8 @@ def tile_edgefeaturenet_pb_kernel(
                     in_=by_partition[:, :, n * BANK * PACK : (n + 1) * BANK * PACK].bitcast(I32),
                 )
 
-        def load_vector(v, vec):
-            nc.sync.dma_start(out=vec_rows[32 * v : 32 * v + 1, :], in_=vec.rearrange("(o n) -> o n", o=1))
+        def load_vector(row, vec):
+            nc.sync.dma_start(out=vec_rows[row : row + 1, :], in_=vec.rearrange("(o n) -> o n", o=1))
 
         load_tokens(0, 1)
         load_tokens(1, 2)
@@ -90,9 +95,10 @@ def tile_edgefeaturenet_pb_kernel(
         nc.sync.dma_start(out=b2_bf16[:], in_=b2.rearrange("(a p t) -> p a t", a=PASSES, t=PACK))
         load_words(w2_words, W2_words)
         load_tokens(2, 4)
-        load_vector(1, b3)
-        load_vector(2, ln_g)
-        load_vector(3, ln_b)
+        load_vector(BIAS_ROW, b3)
+        for row in GAIN_ROWS:
+            load_vector(row, ln_g)
+        load_vector(SHIFT_ROW, ln_b)
         nc.sync.dma_start(out=mask_bf16[:], in_=mask_rows)
         load_scales(w3_planes, W3_scales)
         load_tokens(4, 6)
@@ -112,7 +118,9 @@ def tile_edgefeaturenet_pb_kernel(
         b2_cols = keep.tile([P, PASSES * PACK], F32, name="b2_cols")
         b3_all = keep.tile([P, FEATURES], BF16, name="b3_all")
         gain_all = keep.tile([P, FEATURES], BF16, name="gain_all")
-        shift_all = keep.tile([P, FEATURES], BF16, name="shift_all")
+        coef = keep.tile([P, TILES, P], BF16, name="coef")
+        nc.vector.memset(coef[:], 0.0)
+        port_token = keep.tile([P, 2], BF16, name="port_token")
         mask = keep.tile([P, TILES], F32, name="mask")
 
         w2_sorted = keep.tile([P, PASSES, PASSES * PACK, P], U32, align_bytes=64, name="w2_sorted")
@@ -130,13 +138,13 @@ def tile_edgefeaturenet_pb_kernel(
                 in_=w2_words[:, :, a * K_PASS : (a + 1) * K_PASS].bitcast(I32).rearrange("p g (m t) -> p g t m", t=PACK),
             )
 
-        def spread_vector(v, spread):
+        def spread_vector(row, spread):
             for n in range(HALVES):
                 cols = slice(n * BANK, (n + 1) * BANK)
                 acc = psum_acc.tile([P, BANK], F32, name="acc")
                 nc.tensor.matmul(
                     out=acc[:],
-                    lhsT=ident_bf16[:, 32 * v : 32 * v + 1].to_broadcast([P, P]),
+                    lhsT=ident_bf16[:, row : row + 1].to_broadcast([P, P]),
                     rhs=vec_rows[:, cols],
                     start=True,
                     stop=True,
@@ -148,11 +156,14 @@ def tile_edgefeaturenet_pb_kernel(
 
         xt, x_grouped, x_mx, h_banks, h_planes, h_grouped, h_mx = {}, {}, {}, {}, {}, {}, {}
         y_banks, y, sums, neg_mean, sum_sq, rstd = {}, {}, {}, {}, {}, {}
-        slope, offset, norm, gained = {}, {}, {}, {}
+        slope, offset, rest, gained, coef_bank, coef_rows, rank_banks = {}, {}, {}, {}, {}, {}, {}
 
         def transpose_tokens(i):
             pairs = h1_sb[:, i, :].bitcast(F32)
-            xt[i] = psum_x.tile([P, PASSES, 2, P], F32, name="xt")
+            if i < BORROWED and i % 3 != 0:
+                xt[i] = psum_rank.tile([P, PASSES, 2, P], F32, name="rank")
+            else:
+                xt[i] = psum_x.tile([P, PASSES, 2, P], F32, name="xt")
             for g in range(PASSES):
                 for u in range(2):
                     nc.tensor.transpose(
@@ -198,17 +209,17 @@ def tile_edgefeaturenet_pb_kernel(
                         )
                 h_banks[unit].append(bank)
 
-        def bias_and_relu(unit):
+        def bias_and_relu(unit, t):
             a = unit % PASSES
-            h_planes[unit] = stage.tile([P, PACK, PAIR_TOKENS], BF16, name="h_planes")
-            for t in range(PACK):
-                nc.scalar.activation(
-                    out=h_planes[unit][:, t, :],
-                    in_=h_banks[unit][t // 2][:, t % 2, :],
-                    func=ACT.Relu,
-                    bias=b2_cols[:, PACK * a + t : PACK * a + t + 1],
-                    scale=1.0,
-                )
+            if t == 0:
+                h_planes[unit] = stage.tile([P, PACK, PAIR_TOKENS], BF16, name="h_planes")
+            nc.scalar.activation(
+                out=h_planes[unit][:, t, :],
+                in_=h_banks[unit][t // 2][:, t % 2, :],
+                func=ACT.Relu,
+                bias=b2_cols[:, PACK * a + t : PACK * a + t + 1],
+                scale=1.0,
+            )
 
         def group_hidden(unit):
             h_grouped[unit] = stage.tile([P, PAIR_TOKENS, PACK], BF16, align_bytes=64, name="h_grouped")
@@ -285,42 +296,61 @@ def tile_edgefeaturenet_pb_kernel(
                 scale=1.0 / FEATURES,
             )
 
-        def slope_and_offset(i):
+        def make_slope(i):
             slope[i] = stats.tile([P, 1], F32, name="slope")
-            nc.vector.tensor_scalar(
-                out=slope[i][:], in0=rstd[i][:], scalar1=mask[:, i : i + 1], scalar2=None, op0=ALU.mult
-            )
+            nc.scalar.activation(out=slope[i][:], in_=rstd[i][:], func=ACT.Identity, scale=mask[:, i : i + 1])
+
+        def piece(i, number):
+            return coef[:, i, GAIN_ROWS[number] : GAIN_ROWS[number] + 1]
+
+        def make_offset(i):
             offset[i] = stats.tile([P, 1], F32, name="offset")
-            nc.vector.scalar_tensor_tensor(
-                out=offset[i][:],
-                in0=rstd[i][:],
-                scalar=mask[:, i : i + 1],
-                in1=neg_mean[i][:],
-                op0=ALU.mult,
-                op1=ALU.mult,
-            )
+            nc.scalar.activation(out=offset[i][:], in_=neg_mean[i][:], func=ACT.Identity, scale=slope[i][:, 0:1])
+            nc.scalar.activation(out=piece(i, 0), in_=neg_mean[i][:], func=ACT.Identity, scale=slope[i][:, 0:1])
 
-        def normalise(i):
-            norm[i] = rows.tile([P, FEATURES], F32, name="norm")
-            nc.scalar.activation(
-                out=norm[i][:], in_=y[i][:], func=ACT.Identity, bias=offset[i][:, 0:1], scale=slope[i][:, 0:1]
-            )
+        def second_piece(i):
+            rest[i] = stats.tile([P, 1], F32, name="rest")
+            nc.scalar.activation(out=rest[i][:], in_=piece(i, 0), func=ACT.Identity, bias=offset[i][:, 0:1], scale=-1.0)
+            nc.scalar.activation(out=piece(i, 1), in_=piece(i, 0), func=ACT.Identity, bias=offset[i][:, 0:1], scale=-1.0)
 
-        def gain(i):
+        def third_piece(i):
+            nc.scalar.activation(out=piece(i, 2), in_=piece(i, 1), func=ACT.Identity, bias=rest[i][:, 0:1], scale=-1.0)
+
+        def turn_coefficients(i):
+            coef_bank[i] = psum_coef.tile([P, P], F32, name="coef_bank")
+            nc.tensor.matmul(out=coef_bank[i][:], lhsT=coef[:, i, :], rhs=ident_bf16[:], start=True, stop=True)
+
+        def copy_coefficients(i):
+            coef_rows[i] = stage.tile([P, P], BF16, name="coef_rows")
+            nc.scalar.copy(out=coef_rows[i][:], in_=coef_bank[i][:])
+
+        def outer_products(i):
+            rank_banks[i] = []
+            for n in range(HALVES):
+                bank = psum_rank.tile([P, BANK], F32, name="rank")
+                nc.tensor.matmul(
+                    out=bank[:], lhsT=coef_rows[i][:], rhs=vec_rows[:, n * BANK : (n + 1) * BANK], start=True, stop=True
+                )
+                rank_banks[i].append(bank)
+
+        def gain(i, after_unit):
+            if unit_exists(after_unit):
+                nc.gpsimd.tensor_copy(out=port_token[:, 0:1], in_=h_grouped[after_unit][:, 0, 0:1])
             gained[i] = handover.tile([P, FEATURES], F32, name="gained")
-            engine = nc.gpsimd if i < TILES - GAINS_ON_VECTOR else nc.vector
-            engine.tensor_tensor(out=gained[i][:], in0=norm[i][:], in1=gain_all[:], op=ALU.mult)
+            nc.gpsimd.tensor_tensor(out=gained[i][:], in0=y[i][:], in1=gain_all[:], op=ALU.mult)
 
-        def shift_and_store(i):
+        def scale_shift_and_store(i):
             result = rows.tile([P, FEATURES], F32, name="result")
-            nc.vector.scalar_tensor_tensor(
-                out=result[:],
-                in0=shift_all[:],
-                scalar=mask[:, i : i + 1],
-                in1=gained[i][:],
-                op0=ALU.mult,
-                op1=ALU.add,
-            )
+            for n in range(HALVES):
+                cols = slice(n * BANK, (n + 1) * BANK)
+                nc.vector.scalar_tensor_tensor(
+                    out=result[:, cols],
+                    in0=gained[i][:, cols],
+                    scalar=slope[i][:, 0:1],
+                    in1=rank_banks[i][n][:],
+                    op0=ALU.mult,
+                    op1=ALU.add,
+                )
             nc.sync.dma_start(out=out_rows[:, i, :], in_=result[:])
 
         def tile_exists(i):
@@ -330,50 +360,69 @@ def tile_edgefeaturenet_pb_kernel(
             return 0 <= unit < UNITS
 
         def work_of_slot(s):
-            if unit_exists(s + 2):
-                multiply_first(s + 2)
-            if tile_exists(s + 5):
-                transpose_tokens(s + 5)
+            if tile_exists(s - 3):
+                outer_products(s - 3)
+            if unit_exists(s + 3):
+                multiply_first(s + 3)
             if tile_exists(s - 2):
                 sum_squares(s - 2)
                 inverse_deviation(s - 2)
             if tile_exists(s - 1):
                 add_bias_and_sum(s - 1)
-            if unit_exists(s + 1):
-                group_hidden(s + 1)
-            if unit_exists(s + 2):
-                bias_and_relu(s + 2)
             if tile_exists(s - 2):
-                slope_and_offset(s - 2)
-            if unit_exists(s + 1):
-                quantise_hidden(s + 1)
+                gain(s - 2, s + 2)
+            if unit_exists(s + 3):
+                bias_and_relu(s + 3, 0)
+            if tile_exists(s - 2):
+                make_slope(s - 2)
+            if unit_exists(s + 3):
+                bias_and_relu(s + 3, 1)
+            if tile_exists(s - 2):
+                make_offset(s - 2)
+            if unit_exists(s + 3):
+                bias_and_relu(s + 3, 2)
+            if tile_exists(s - 2):
+                second_piece(s - 2)
+            if unit_exists(s + 3):
+                bias_and_relu(s + 3, 3)
+            if tile_exists(s - 2):
+                third_piece(s - 2)
+            if tile_exists(s - 3):
+                scale_shift_and_store(s - 3)
+            if tile_exists(s - 1):
+                mean(s - 1)
+            if tile_exists(s + 6):
+                transpose_tokens(s + 6)
             if tile_exists(s):
                 multiply_second(s)
             if tile_exists(s - 2):
-                normalise(s - 2)
-                gain(s - 2)
-            if tile_exists(s - 3):
-                shift_and_store(s - 3)
-            if tile_exists(s + 5):
-                group_tokens(s + 5)
-            if tile_exists(s - 1):
-                mean(s - 1)
-            if (s + 3) % PAIR == 0 and 0 <= (s + 3) // PAIR < PAIRS:
-                quantise_tokens((s + 3) // PAIR)
+                turn_coefficients(s - 2)
+            if unit_exists(s + 2):
+                quantise_hidden(s + 2)
+            if (s + 4) % PAIR == 0 and 0 <= (s + 4) // PAIR < PAIRS:
+                quantise_tokens((s + 4) // PAIR)
+            if unit_exists(s + 3):
+                group_hidden(s + 3)
+            if tile_exists(s + 6):
+                group_tokens(s + 6)
+            if tile_exists(s - 2):
+                copy_coefficients(s - 2)
 
+        work_of_slot(-6)
         work_of_slot(-5)
-        work_of_slot(-4)
         nc.vector.tensor_copy(out=b2_cols[:], in_=b2_bf16[:].rearrange("p a t -> p (a t)"))
         sort_scales()
         sort_words(0)
-        work_of_slot(-3)
+        work_of_slot(-4)
         sort_words(1)
-        work_of_slot(-2)
-        spread_vector(1, b3_all)
+        work_of_slot(-3)
         nc.vector.tensor_copy(out=mask[:], in_=mask_bf16[:])
+        nc.vector.tensor_copy(
+            out=coef[:, :, SHIFT_ROW : SHIFT_ROW + 1], in_=mask_bf16[:].rearrange("p (i o) -> p i o", o=1)
+        )
+        work_of_slot(-2)
+        spread_vector(BIAS_ROW, b3_all)
         work_of_slot(-1)
-        spread_vector(2, gain_all)
-        work_of_slot(0)
-        spread_vector(3, shift_all)
-        for s in range(1, TILES + 4):
+        spread_vector(GAIN_ROWS[0], gain_all)
+        for s in range(0, TILES + 4):
             work_of_slot(s)

@@ -48,7 +48,7 @@ def tile_edgefeaturenet_pb_kernel(
         stage = stack.enter_context(tc.tile_pool(name="stage", bufs=4))
         rows = stack.enter_context(tc.tile_pool(name="rows", bufs=4))
         stats = stack.enter_context(tc.tile_pool(name="stats", bufs=4))
-        handover = stack.enter_context(tc.tile_pool(name="handover", bufs=3))
+        handover = stack.enter_context(tc.tile_pool(name="handover", bufs=4))
         psum_x = stack.enter_context(tc.psum_pool(name="psum_x", bufs=1))
         psum_h = stack.enter_context(tc.psum_pool(name="psum_h", bufs=2))
         psum_acc = stack.enter_context(tc.psum_pool(name="psum_acc", bufs=2))
@@ -361,16 +361,23 @@ def tile_edgefeaturenet_pb_kernel(
 
         def work_of_slot(s):
             if tile_exists(s - 3):
-                outer_products(s - 3)
+                turn_coefficients(s - 3)
             if unit_exists(s + 3):
                 multiply_first(s + 3)
+            if tile_exists(s + 6):
+                transpose_tokens(s + 6)
             if tile_exists(s - 2):
                 sum_squares(s - 2)
-                inverse_deviation(s - 2)
+            if tile_exists(s - 4):
+                scale_shift_and_store(s - 4)
+            if tile_exists(s - 3):
+                copy_coefficients(s - 3)
+                outer_products(s - 3)
             if tile_exists(s - 1):
                 add_bias_and_sum(s - 1)
             if tile_exists(s - 2):
                 gain(s - 2, s + 2)
+                inverse_deviation(s - 2)
             if unit_exists(s + 3):
                 bias_and_relu(s + 3, 0)
             if tile_exists(s - 2):
@@ -387,16 +394,10 @@ def tile_edgefeaturenet_pb_kernel(
                 bias_and_relu(s + 3, 3)
             if tile_exists(s - 2):
                 third_piece(s - 2)
-            if tile_exists(s - 3):
-                scale_shift_and_store(s - 3)
             if tile_exists(s - 1):
                 mean(s - 1)
-            if tile_exists(s + 6):
-                transpose_tokens(s + 6)
             if tile_exists(s):
                 multiply_second(s)
-            if tile_exists(s - 2):
-                turn_coefficients(s - 2)
             if unit_exists(s + 2):
                 quantise_hidden(s + 2)
             if (s + 4) % PAIR == 0 and 0 <= (s + 4) // PAIR < PAIRS:
@@ -405,8 +406,6 @@ def tile_edgefeaturenet_pb_kernel(
                 group_hidden(s + 3)
             if tile_exists(s + 6):
                 group_tokens(s + 6)
-            if tile_exists(s - 2):
-                copy_coefficients(s - 2)
 
         work_of_slot(-6)
         work_of_slot(-5)
@@ -424,5 +423,5 @@ def tile_edgefeaturenet_pb_kernel(
         spread_vector(BIAS_ROW, b3_all)
         work_of_slot(-1)
         spread_vector(GAIN_ROWS[0], gain_all)
-        for s in range(0, TILES + 4):
+        for s in range(0, TILES + 5):
             work_of_slot(s)

@@ -120,7 +120,7 @@ def tile_edgefeaturenet_pb_kernel(
         gain_all = keep.tile([P, FEATURES], BF16, name="gain_all")
         coef = keep.tile([P, TILES, P], BF16, name="coef")
         nc.vector.memset(coef[:], 0.0)
-        port_token = keep.tile([P, 2], BF16, name="port_token")
+        port_token = keep.tile([P, 1], U32, name="port_token")
         mask = keep.tile([P, TILES], F32, name="mask")
 
         w2_sorted = keep.tile([P, PASSES, PASSES * PACK, P], U32, align_bytes=64, name="w2_sorted")
@@ -335,7 +335,7 @@ def tile_edgefeaturenet_pb_kernel(
 
         def gain(i, after_unit):
             if unit_exists(after_unit):
-                nc.gpsimd.tensor_copy(out=port_token[:, 0:1], in_=h_grouped[after_unit][:, 0, 0:1])
+                nc.gpsimd.tensor_copy(out=port_token[:], in_=h_mx[after_unit][0][:, 0:1])
             gained[i] = handover.tile([P, FEATURES], F32, name="gained")
             nc.gpsimd.tensor_tensor(out=gained[i][:], in0=y[i][:], in1=gain_all[:], op=ALU.mult)
 
@@ -376,7 +376,7 @@ def tile_edgefeaturenet_pb_kernel(
             if tile_exists(s - 1):
                 add_bias_and_sum(s - 1)
             if tile_exists(s - 2):
-                gain(s - 2, s + 2)
+                gain(s - 2, s + 1)
                 inverse_deviation(s - 2)
             if unit_exists(s + 3):
                 bias_and_relu(s + 3, 0)
@@ -398,10 +398,10 @@ def tile_edgefeaturenet_pb_kernel(
                 mean(s - 1)
             if tile_exists(s):
                 multiply_second(s)
-            if unit_exists(s + 2):
-                quantise_hidden(s + 2)
             if (s + 4) % PAIR == 0 and 0 <= (s + 4) // PAIR < PAIRS:
                 quantise_tokens((s + 4) // PAIR)
+            if unit_exists(s + 2):
+                quantise_hidden(s + 2)
             if unit_exists(s + 3):
                 group_hidden(s + 3)
             if tile_exists(s + 6):

@@ -120,7 +120,8 @@ def tile_edgefeaturenet_pb_kernel(
         gain_all = keep.tile([P, FEATURES], BF16, name="gain_all")
         coef = keep.tile([P, TILES, P], BF16, name="coef")
         nc.vector.memset(coef[:], 0.0)
-        port_token = keep.tile([P, 1], U32, name="port_token")
+        port_word = keep.tile([P, 1], U32, name="port_word")
+        port_value = keep.tile([P, 1], F32, name="port_value")
         mask = keep.tile([P, TILES], F32, name="mask")
 
         w2_sorted = keep.tile([P, PASSES, PASSES * PACK, P], U32, align_bytes=64, name="w2_sorted")
@@ -333,9 +334,13 @@ def tile_edgefeaturenet_pb_kernel(
                 )
                 rank_banks[i].append(bank)
 
-        def gain(i, after_unit):
-            if unit_exists(after_unit):
-                nc.gpsimd.tensor_copy(out=port_token[:], in_=h_mx[after_unit][0][:, 0:1])
+        def gain(i, s):
+            before = s - 1
+            if unit_exists(before + 3):
+                if pair_quantised_in(before) is not None:
+                    nc.gpsimd.tensor_copy(out=port_word[:], in_=x_mx[pair_quantised_in(before)][0][:, 0:1])
+                else:
+                    nc.gpsimd.tensor_copy(out=port_value[:], in_=neg_mean[before - 1][:])
             gained[i] = handover.tile([P, FEATURES], F32, name="gained")
             nc.gpsimd.tensor_tensor(out=gained[i][:], in0=y[i][:], in1=gain_all[:], op=ALU.mult)
 
@@ -359,6 +364,10 @@ def tile_edgefeaturenet_pb_kernel(
         def unit_exists(unit):
             return 0 <= unit < UNITS
 
+        def pair_quantised_in(s):
+            q, odd = divmod(s + 4, PAIR)
+            return q if odd == 0 and 0 <= q < PAIRS else None
+
         def work_of_slot(s):
             if tile_exists(s - 3):
                 turn_coefficients(s - 3)
@@ -376,7 +385,7 @@ def tile_edgefeaturenet_pb_kernel(
             if tile_exists(s - 1):
                 add_bias_and_sum(s - 1)
             if tile_exists(s - 2):
-                gain(s - 2, s + 1)
+                gain(s - 2, s)
                 inverse_deviation(s - 2)
             if unit_exists(s + 3):
                 bias_and_relu(s + 3, 0)
@@ -398,8 +407,8 @@ def tile_edgefeaturenet_pb_kernel(
                 mean(s - 1)
             if tile_exists(s):
                 multiply_second(s)
-            if (s + 4) % PAIR == 0 and 0 <= (s + 4) // PAIR < PAIRS:
-                quantise_tokens((s + 4) // PAIR)
+            if pair_quantised_in(s) is not None:
+                quantise_tokens(pair_quantised_in(s))
             if unit_exists(s + 2):
                 quantise_hidden(s + 2)
             if unit_exists(s + 3):

@@ -224,7 +224,10 @@ def tile_edgefeaturenet_pb_kernel(
 
         def group_hidden(unit):
             h_grouped[unit] = stage.tile([P, PAIR_TOKENS, PACK], BF16, align_bytes=64, name="h_grouped")
-            nc.vector.tensor_copy(out=h_grouped[unit][:], in_=h_planes[unit][:].rearrange("p t r -> p r t"))
+            nc.vector.tensor_copy(
+                out=h_grouped[unit][:].rearrange("p (c i) t -> p c t i", i=4),
+                in_=h_planes[unit][:].rearrange("p t (c i) -> p c t i", i=4),
+            )
 
         def quantise_hidden(unit):
             h_mx[unit] = quantise(h_grouped[unit][:].rearrange("p r t -> p (r t)"), PAIR_TOKENS, "_h")

@@ -120,7 +120,6 @@ def tile_edgefeaturenet_pb_kernel(
         gain_all = keep.tile([P, FEATURES], BF16, name="gain_all")
         coef = keep.tile([P, TILES, P], BF16, name="coef")
         nc.vector.memset(coef[:], 0.0)
-        port_word = keep.tile([P, 1], U32, name="port_word")
         port_value = keep.tile([P, 1], F32, name="port_value")
         mask = keep.tile([P, TILES], F32, name="mask")
 
@@ -223,24 +222,26 @@ def tile_edgefeaturenet_pb_kernel(
             )
 
         def group_hidden(unit):
-            h_grouped[unit] = stage.tile([P, PAIR_TOKENS, PACK], BF16, align_bytes=64, name="h_grouped")
+            q, a = divmod(unit, PASSES)
+            if a == 0:
+                h_grouped[q] = stage.tile([P, PASSES, PAIR_TOKENS, PACK], BF16, align_bytes=64, name="h_grouped")
             nc.vector.tensor_copy(
-                out=h_grouped[unit][:].rearrange("p (c i) t -> p c t i", i=4),
+                out=h_grouped[q][:, a, :, :].rearrange("p (c i) t -> p c t i", i=4),
                 in_=h_planes[unit][:].rearrange("p t (c i) -> p c t i", i=4),
             )
 
-        def quantise_hidden(unit):
-            h_mx[unit] = quantise(h_grouped[unit][:].rearrange("p r t -> p (r t)"), PAIR_TOKENS, "_h")
+        def quantise_hidden(q):
+            h_mx[q] = quantise(h_grouped[q][:].rearrange("p a r t -> p (a r t)"), PASSES * PAIR_TOKENS, "_h")
 
         def multiply_second(i):
             q, j = divmod(i, PAIR)
-            tokens = slice(j * P, (j + 1) * P)
+            codes, scales = h_mx[q]
             y_banks[i] = []
             for n in range(HALVES):
                 cols = slice(n * BANK, (n + 1) * BANK)
                 acc = psum_acc.tile([P, BANK], F32, name="acc")
                 for a in range(PASSES):
-                    codes, scales = h_mx[PASSES * q + a]
+                    tokens = slice(a * PAIR_TOKENS + j * P, a * PAIR_TOKENS + (j + 1) * P)
                     nc.tensor.matmul_mx(
                         out=acc[:],
                         lhsT=codes[:, tokens].bitcast(FP8X4),
@@ -269,13 +270,9 @@ def tile_edgefeaturenet_pb_kernel(
 
         def mean(i):
             neg_mean[i] = stats.tile([P, 1], F32, name="neg_mean")
-            nc.vector.tensor_scalar(
-                out=neg_mean[i][:],
-                in0=sums[i][:, 0:1],
-                scalar1=sums[i][:, 1:2],
-                scalar2=-1.0 / FEATURES,
-                op0=ALU.add,
-                op1=ALU.mult,
+            scaled = stats.tile([P, HALVES], F32, name="scaled")
+            nc.scalar.activation(
+                out=scaled[:], in_=sums[i][:], func=ACT.Identity, scale=-1.0 / FEATURES, accum_out=neg_mean[i][:]
             )
 
         def sum_squares(i):
@@ -340,10 +337,7 @@ def tile_edgefeaturenet_pb_kernel(
         def gain(i, s):
             before = s - 1
             if unit_exists(before + 3):
-                if pair_quantised_in(before) is not None:
-                    nc.gpsimd.tensor_copy(out=port_word[:], in_=x_mx[pair_quantised_in(before)][0][:, 0:1])
-                else:
-                    nc.gpsimd.tensor_copy(out=port_value[:], in_=neg_mean[before - 1][:])
+                nc.gpsimd.tensor_copy(out=port_value[:], in_=sums[before - 1][:, HALVES - 1 : HALVES])
             gained[i] = handover.tile([P, FEATURES], F32, name="gained")
             nc.gpsimd.tensor_tensor(out=gained[i][:], in0=y[i][:], in1=gain_all[:], op=ALU.mult)
 
@@ -359,13 +353,20 @@ def tile_edgefeaturenet_pb_kernel(
                     op0=ALU.mult,
                     op1=ALU.add,
                 )
-            nc.sync.dma_start(out=out_rows[:, i, :], in_=result[:])
+                if i == TILES - 1:
+                    nc.sync.dma_start(out=out_rows[:, i, cols], in_=result[:, cols])
+            if i < TILES - 1:
+                nc.sync.dma_start(out=out_rows[:, i, :], in_=result[:])
 
         def tile_exists(i):
             return 0 <= i < TILES
 
         def unit_exists(unit):
             return 0 <= unit < UNITS
+
+        def hidden_pair_quantised_in(s):
+            q, odd = divmod(s + 1, PAIR)
+            return q if odd == 0 and 0 <= q < PAIRS else None
 
         def pair_quantised_in(s):
             q, odd = divmod(s + 4, PAIR)
@@ -380,12 +381,14 @@ def tile_edgefeaturenet_pb_kernel(
                 transpose_tokens(s + 6)
             if tile_exists(s - 2):
                 sum_squares(s - 2)
+            if tile_exists(s - 1) and not tile_exists(s):
+                add_bias_and_sum(s - 1)
             if tile_exists(s - 4):
                 scale_shift_and_store(s - 4)
             if tile_exists(s - 3):
                 copy_coefficients(s - 3)
                 outer_products(s - 3)
-            if tile_exists(s - 1):
+            if tile_exists(s - 1) and tile_exists(s):
                 add_bias_and_sum(s - 1)
             if tile_exists(s - 2):
                 gain(s - 2, s)
@@ -406,18 +409,18 @@ def tile_edgefeaturenet_pb_kernel(
                 bias_and_relu(s + 3, 3)
             if tile_exists(s - 2):
                 third_piece(s - 2)
-            if tile_exists(s - 1):
-                mean(s - 1)
             if tile_exists(s):
                 multiply_second(s)
             if pair_quantised_in(s) is not None:
                 quantise_tokens(pair_quantised_in(s))
-            if unit_exists(s + 2):
-                quantise_hidden(s + 2)
+            if hidden_pair_quantised_in(s) is not None:
+                quantise_hidden(hidden_pair_quantised_in(s))
             if unit_exists(s + 3):
                 group_hidden(s + 3)
             if tile_exists(s + 6):
                 group_tokens(s + 6)
+            if tile_exists(s - 1):
+                mean(s - 1)
 
         work_of_slot(-6)
         work_of_slot(-5)

@@ -156,7 +156,7 @@ def tile_edgefeaturenet_pb_kernel(
 
         xt, x_grouped, x_mx, h_banks, h_planes, h_grouped, h_mx = {}, {}, {}, {}, {}, {}, {}
         y_banks, y, sums, neg_mean, sum_sq, rstd = {}, {}, {}, {}, {}, {}
-        slope, offset, rest, gained, coef_bank, coef_rows, rank_banks = {}, {}, {}, {}, {}, {}, {}
+        slope, offset, rest, gained, coef_bank, coef_rows, rank_banks, results = {}, {}, {}, {}, {}, {}, {}, {}
 
         def transpose_tokens(i):
             pairs = h1_sb[:, i, :].bitcast(F32)
@@ -337,12 +337,16 @@ def tile_edgefeaturenet_pb_kernel(
         def gain(i, s):
             before = s - 1
             if unit_exists(before + 3):
-                nc.gpsimd.tensor_copy(out=port_value[:], in_=sums[before - 1][:, HALVES - 1 : HALVES])
+                if tile_exists(before - 4):
+                    nc.gpsimd.tensor_copy(out=port_value[:], in_=results[before - 4][:, FEATURES - 1 : FEATURES])
+                else:
+                    nc.gpsimd.tensor_copy(out=port_value[:], in_=sums[before - 1][:, HALVES - 1 : HALVES])
             gained[i] = handover.tile([P, FEATURES], F32, name="gained")
             nc.gpsimd.tensor_tensor(out=gained[i][:], in0=y[i][:], in1=gain_all[:], op=ALU.mult)
 
         def scale_shift_and_store(i):
             result = rows.tile([P, FEATURES], F32, name="result")
+            results[i] = result
             for n in range(HALVES):
                 cols = slice(n * BANK, (n + 1) * BANK)
                 nc.vector.scalar_tensor_tensor(
@@ -381,15 +385,15 @@ def tile_edgefeaturenet_pb_kernel(
                 transpose_tokens(s + 6)
             if tile_exists(s - 2):
                 sum_squares(s - 2)
-            if tile_exists(s - 1) and not tile_exists(s):
+            if tile_exists(s - 1):
                 add_bias_and_sum(s - 1)
+            if tile_exists(s):
+                multiply_second(s)
             if tile_exists(s - 4):
                 scale_shift_and_store(s - 4)
             if tile_exists(s - 3):
                 copy_coefficients(s - 3)
                 outer_products(s - 3)
-            if tile_exists(s - 1) and tile_exists(s):
-                add_bias_and_sum(s - 1)
             if tile_exists(s - 2):
                 gain(s - 2, s)
                 inverse_deviation(s - 2)
@@ -409,8 +413,6 @@ def tile_edgefeaturenet_pb_kernel(
                 bias_and_relu(s + 3, 3)
             if tile_exists(s - 2):
                 third_piece(s - 2)
-            if tile_exists(s):
-                multiply_second(s)
             if pair_quantised_in(s) is not None:
                 quantise_tokens(pair_quantised_in(s))
             if hidden_pair_quantised_in(s) is not None:

@@ -396,21 +396,24 @@ def tile_edgefeaturenet_pb_kernel(
                 outer_products(s - 3)
             if tile_exists(s - 2):
                 gain(s - 2, s)
-                inverse_deviation(s - 2)
             if unit_exists(s + 3):
                 bias_and_relu(s + 3, 0)
             if tile_exists(s - 2):
-                make_slope(s - 2)
+                inverse_deviation(s - 2)
             if unit_exists(s + 3):
                 bias_and_relu(s + 3, 1)
             if tile_exists(s - 2):
-                make_offset(s - 2)
+                make_slope(s - 2)
             if unit_exists(s + 3):
                 bias_and_relu(s + 3, 2)
             if tile_exists(s - 2):
-                second_piece(s - 2)
+                make_offset(s - 2)
             if unit_exists(s + 3):
                 bias_and_relu(s + 3, 3)
+            if tile_exists(s - 2):
+                second_piece(s - 2)
+            if tile_exists(s - 1):
+                mean(s - 1)
             if tile_exists(s - 2):
                 third_piece(s - 2)
             if pair_quantised_in(s) is not None:
@@ -421,8 +424,6 @@ def tile_edgefeaturenet_pb_kernel(
                 group_hidden(s + 3)
             if tile_exists(s + 6):
                 group_tokens(s + 6)
-            if tile_exists(s - 1):
-                mean(s - 1)
 
         work_of_slot(-6)
         work_of_slot(-5)

@@ -29,6 +29,7 @@ EPS = 1e-5
 GAIN_ROWS = (0, 2, 3)
 SHIFT_ROW = 4
 BIAS_ROW = 32
+WARMING_MATMULS = 6
 BORROWED = 9
 
 FLOPS = 2 * 2 * TOKENS * FEATURES * FEATURES
@@ -427,6 +428,15 @@ def tile_edgefeaturenet_pb_kernel(
 
         work_of_slot(-6)
         work_of_slot(-5)
+        for dummy in range(WARMING_MATMULS):
+            idle_bank = psum_acc.tile([P, BANK], F32, name="acc")
+            nc.tensor.matmul(
+                out=idle_bank[:],
+                lhsT=ident_bf16[:],
+                rhs=coef[:, 0 : BANK // P, :].rearrange("p i c -> p (i c)"),
+                start=True,
+                stop=True,
+            )
         nc.vector.tensor_copy(out=b2_cols[:], in_=b2_bf16[:].rearrange("p a t -> p (a t)"))
         sort_scales()
         sort_words(0)

@@ -29,6 +29,7 @@ EPS = 1e-5
 GAIN_ROWS = (0, 2, 3)
 SHIFT_ROW = 4
 BIAS_ROW = 32
+LATE_WARMING_MATMULS = {TILES - 3: 2, TILES - 2: 3}
 WARMING_MATMULS = 6
 BORROWED = 9
 
@@ -55,6 +56,14 @@ def tile_edgefeaturenet_pb_kernel(
         psum_acc = stack.enter_context(tc.psum_pool(name="psum_acc", bufs=2))
         psum_rank = stack.enter_context(tc.psum_pool(name="psum_rank", bufs=2))
         psum_coef = stack.enter_context(tc.psum_pool(name="psum_coef", bufs=1))
+
+        zeros = keep.tile([P, BANK], BF16, name="zeros")
+        nc.gpsimd.memset(zeros[:], 0.0)
+
+        def warm_tensor_engine(count):
+            for dummy in range(count):
+                idle_bank = psum_acc.tile([P, BANK], F32, name="acc")
+                nc.tensor.matmul(out=idle_bank[:], lhsT=zeros[:, 0:P], rhs=zeros[:], start=True, stop=True)
 
         h1_sb = keep.tile([P, TILES, FEATURES], BF16, name="h1_sb")
         w2_words = keep.tile([P, PASSES, FEATURES], U32, align_bytes=64, name="w2_words")
@@ -348,18 +357,22 @@ def tile_edgefeaturenet_pb_kernel(
         def scale_shift_and_store(i):
             result = rows.tile([P, FEATURES], F32, name="result")
             results[i] = result
+            pieces_of_bank = 2 if i == TILES - 1 else 1
+            width = BANK // pieces_of_bank
             for n in range(HALVES):
-                cols = slice(n * BANK, (n + 1) * BANK)
-                nc.vector.scalar_tensor_tensor(
-                    out=result[:, cols],
-                    in0=gained[i][:, cols],
-                    scalar=slope[i][:, 0:1],
-                    in1=rank_banks[i][n][:],
-                    op0=ALU.mult,
-                    op1=ALU.add,
-                )
-                if i == TILES - 1:
-                    nc.sync.dma_start(out=out_rows[:, i, cols], in_=result[:, cols])
+                for piece_number in range(pieces_of_bank):
+                    in_bank = slice(piece_number * width, (piece_number + 1) * width)
+                    cols = slice(n * BANK + piece_number * width, n * BANK + (piece_number + 1) * width)
+                    nc.vector.scalar_tensor_tensor(
+                        out=result[:, cols],
+                        in0=gained[i][:, cols],
+                        scalar=slope[i][:, 0:1],
+                        in1=rank_banks[i][n][:, in_bank],
+                        op0=ALU.mult,
+                        op1=ALU.add,
+                    )
+                    if i == TILES - 1:
+                        nc.sync.dma_start(out=out_rows[:, i, cols], in_=result[:, cols])
             if i < TILES - 1:
                 nc.sync.dma_start(out=out_rows[:, i, :], in_=result[:])
 
@@ -395,6 +408,7 @@ def tile_edgefeaturenet_pb_kernel(
             if tile_exists(s - 3):
                 copy_coefficients(s - 3)
                 outer_products(s - 3)
+                warm_tensor_engine(LATE_WARMING_MATMULS.get(s - 3, 0))
             if tile_exists(s - 2):
                 gain(s - 2, s)
             if unit_exists(s + 3):
@@ -428,15 +442,7 @@ def tile_edgefeaturenet_pb_kernel(
 
         work_of_slot(-6)
         work_of_slot(-5)
-        for dummy in range(WARMING_MATMULS):
-            idle_bank = psum_acc.tile([P, BANK], F32, name="acc")
-            nc.tensor.matmul(
-                out=idle_bank[:],
-                lhsT=ident_bf16[:],
-                rhs=coef[:, 0 : BANK // P, :].rearrange("p i c -> p (i c)"),
-                start=True,
-                stop=True,
-            )
+        warm_tensor_engine(WARMING_MATMULS)
         nc.vector.tensor_copy(out=b2_cols[:], in_=b2_bf16[:].rearrange("p a t -> p (a t)"))
         sort_scales()
         sort_words(0)

@@ -29,8 +29,9 @@ EPS = 1e-5
 GAIN_ROWS = (0, 2, 3)
 SHIFT_ROW = 4
 BIAS_ROW = 32
-LATE_WARMING_MATMULS = {TILES - 3: 2, TILES - 2: 3}
-WARMING_MATMULS = 6
+LATE_WARMING_MATMULS = {TILES - 3: 2}
+WARMING_MATMULS = 4
+LATE_TILES = 4
 BORROWED = 9
 
 FLOPS = 2 * 2 * TOKENS * FEATURES * FEATURES
@@ -66,7 +67,10 @@ def tile_edgefeaturenet_pb_kernel(
                 nc.tensor.matmul(out=idle_bank[:], lhsT=zeros[:, 0:P], rhs=zeros[:], start=True, stop=True)
 
         h1_sb = keep.tile([P, TILES, FEATURES], BF16, name="h1_sb")
-        w2_words = keep.tile([P, PASSES, FEATURES], U32, align_bytes=64, name="w2_words")
+        w2_words = [
+            keep.tile([P, PASSES, BANK], U32, align_bytes=64, name="w2_words_0"),
+            keep.tile([P, PASSES, BANK], U32, align_bytes=64, name="w2_words_1"),
+        ]
         w3_words = keep.tile([P, PASSES, FEATURES], U32, align_bytes=64, name="w3_words")
         w2_planes = keep.tile([P, FEATURES], U8, align_bytes=64, name="w2_planes")
         nc.vector.memset(w2_planes[:].bitcast(I32), 0)
@@ -103,7 +107,12 @@ def tile_edgefeaturenet_pb_kernel(
         load_tokens(1, 2)
         load_scales(w2_planes, W2_scales)
         nc.sync.dma_start(out=b2_bf16[:], in_=b2.rearrange("(a p t) -> p a t", a=PASSES, t=PACK))
-        load_words(w2_words, W2_words)
+        w2_by_partition = W2_words.rearrange("g p n t -> p g (n t)")
+        for n in range(HALVES):
+            nc.sync.dma_start(
+                out=w2_words[n][:].bitcast(I32),
+                in_=w2_by_partition[:, :, n * BANK * PACK : (n + 1) * BANK * PACK].bitcast(I32),
+            )
         load_tokens(2, 4)
         load_vector(BIAS_ROW, b3)
         for row in GAIN_ROWS:
@@ -113,7 +122,8 @@ def tile_edgefeaturenet_pb_kernel(
         load_scales(w3_planes, W3_scales)
         load_tokens(4, 6)
         load_words(w3_words, W3_words)
-        load_tokens(6, 10)
+        load_tokens(6, 7)
+        load_tokens(7, 10)
         load_tokens(10, TILES)
 
         ident_f32 = keep.tile([P, P], F32, name="ident_f32")
@@ -145,7 +155,7 @@ def tile_edgefeaturenet_pb_kernel(
         def sort_words(a):
             nc.vector.tensor_copy(
                 out=w2_sorted[:, :, PACK * a : PACK * (a + 1), :].bitcast(I32),
-                in_=w2_words[:, :, a * K_PASS : (a + 1) * K_PASS].bitcast(I32).rearrange("p g (m t) -> p g t m", t=PACK),
+                in_=w2_words[a][:].bitcast(I32).rearrange("p g (m t) -> p g t m", t=PACK),
             )
 
         def spread_vector(row, spread):
@@ -165,7 +175,7 @@ def tile_edgefeaturenet_pb_kernel(
                     nc.scalar.copy(out=spread[:, cols], in_=acc[:])
 
         xt, x_grouped, x_mx, h_banks, h_planes, h_grouped, h_mx = {}, {}, {}, {}, {}, {}, {}
-        y_banks, y, sums, neg_mean, sum_sq, rstd = {}, {}, {}, {}, {}, {}
+        y_banks, y, sums, neg_mean, sum_sq, rstd, mean_and_variance = {}, {}, {}, {}, {}, {}, {}
         slope, offset, rest, gained, coef_bank, coef_rows, rank_banks, results = {}, {}, {}, {}, {}, {}, {}, {}
 
         def transpose_tokens(i):
@@ -275,8 +285,19 @@ def tile_edgefeaturenet_pb_kernel(
                     in1=b3_all[:, cols],
                     op0=ALU.mult,
                     op1=ALU.add,
-                    accum_out=sums[i][:, n : n + 1],
+                    accum_out=sums[i][:, n : n + 1] if i < TILES - 1 else None,
                 )
+
+        def statistics_on_vector(i):
+            partial = stats.tile([P, HALVES, 6], F32, name="partial")
+            for n in range(HALVES):
+                nc.vector.bn_stats(out=partial[:, n, :], in_=y[i][:, n * BANK : (n + 1) * BANK])
+            mean_and_variance[i] = stats.tile([P, 2], F32, name="mean_and_variance")
+            nc.vector.bn_aggr(out=mean_and_variance[i][:], in_=partial[:].rearrange("p n c -> p (n c)"))
+            neg_mean[i] = stats.tile([P, 1], F32, name="neg_mean")
+            nc.vector.tensor_scalar(
+                out=neg_mean[i][:], in0=mean_and_variance[i][:, 0:1], scalar1=-1.0, scalar2=None, op0=ALU.mult
+            )
 
         def mean(i):
             neg_mean[i] = stats.tile([P, 1], F32, name="neg_mean")
@@ -299,13 +320,22 @@ def tile_edgefeaturenet_pb_kernel(
 
         def inverse_deviation(i):
             rstd[i] = stats.tile([P, 1], F32, name="rstd")
-            nc.scalar.activation(
-                out=rstd[i][:],
-                in_=sum_sq[i][:],
-                func=ACT.Abs_reciprocal_sqrt,
-                bias=eps[:, 0:1],
-                scale=1.0 / FEATURES,
-            )
+            if i == TILES - 1:
+                nc.scalar.activation(
+                    out=rstd[i][:],
+                    in_=mean_and_variance[i][:, 1:2],
+                    func=ACT.Abs_reciprocal_sqrt,
+                    bias=eps[:, 0:1],
+                    scale=1.0,
+                )
+            else:
+                nc.scalar.activation(
+                    out=rstd[i][:],
+                    in_=sum_sq[i][:],
+                    func=ACT.Abs_reciprocal_sqrt,
+                    bias=eps[:, 0:1],
+                    scale=1.0 / FEATURES,
+                )
 
         def make_slope(i):
             slope[i] = stats.tile([P, 1], F32, name="slope")
@@ -338,7 +368,12 @@ def tile_edgefeaturenet_pb_kernel(
         def outer_products(i):
             rank_banks[i] = []
             for n in range(HALVES):
-                bank = psum_rank.tile([P, BANK], F32, name="rank")
+                if i == TILES - 3:
+                    bank = psum_h.tile([P, BANK], F32, name="hb")
+                elif i == TILES - 1:
+                    bank = psum_acc.tile([P, BANK], F32, name="acc")
+                else:
+                    bank = psum_rank.tile([P, BANK], F32, name="rank")
                 nc.tensor.matmul(
                     out=bank[:], lhsT=coef_rows[i][:], rhs=vec_rows[:, n * BANK : (n + 1) * BANK], start=True, stop=True
                 )
@@ -371,9 +406,9 @@ def tile_edgefeaturenet_pb_kernel(
                         op0=ALU.mult,
                         op1=ALU.add,
                     )
-                    if i == TILES - 1:
+                    if i >= TILES - LATE_TILES:
                         nc.sync.dma_start(out=out_rows[:, i, cols], in_=result[:, cols])
-            if i < TILES - 1:
+            if i < TILES - LATE_TILES:
                 nc.sync.dma_start(out=out_rows[:, i, :], in_=result[:])
 
         def tile_exists(i):
@@ -381,6 +416,13 @@ def tile_edgefeaturenet_pb_kernel(
 
         def unit_exists(unit):
             return 0 <= unit < UNITS
+
+        def tiles_turned_in(s):
+            if s == -4:
+                return []
+            if s == -3:
+                return [2, 3]
+            return [s + 6] if tile_exists(s + 6) else []
 
         def hidden_pair_quantised_in(s):
             q, odd = divmod(s + 1, PAIR)
@@ -395,12 +437,17 @@ def tile_edgefeaturenet_pb_kernel(
                 turn_coefficients(s - 3)
             if unit_exists(s + 3):
                 multiply_first(s + 3)
-            if tile_exists(s + 6):
-                transpose_tokens(s + 6)
-            if tile_exists(s - 2):
+            for i in tiles_turned_in(s):
+                transpose_tokens(i)
+            if tile_exists(s - 2) and s - 2 < TILES - 1:
                 sum_squares(s - 2)
+            if s - 2 == TILES - 1:
+                inverse_deviation(s - 2)
+                make_slope(s - 2)
             if tile_exists(s - 1):
                 add_bias_and_sum(s - 1)
+            if s - 1 == TILES - 1:
+                statistics_on_vector(s - 1)
             if tile_exists(s):
                 multiply_second(s)
             if tile_exists(s - 4):
@@ -413,11 +460,11 @@ def tile_edgefeaturenet_pb_kernel(
                 gain(s - 2, s)
             if unit_exists(s + 3):
                 bias_and_relu(s + 3, 0)
-            if tile_exists(s - 2):
+            if tile_exists(s - 2) and s - 2 < TILES - 1:
                 inverse_deviation(s - 2)
             if unit_exists(s + 3):
                 bias_and_relu(s + 3, 1)
-            if tile_exists(s - 2):
+            if tile_exists(s - 2) and s - 2 < TILES - 1:
                 make_slope(s - 2)
             if unit_exists(s + 3):
                 bias_and_relu(s + 3, 2)
@@ -427,7 +474,7 @@ def tile_edgefeaturenet_pb_kernel(
                 bias_and_relu(s + 3, 3)
             if tile_exists(s - 2):
                 second_piece(s - 2)
-            if tile_exists(s - 1):
+            if tile_exists(s - 1) and s - 1 < TILES - 1:
                 mean(s - 1)
             if tile_exists(s - 2):
                 third_piece(s - 2)
@@ -437,8 +484,8 @@ def tile_edgefeaturenet_pb_kernel(
                 quantise_hidden(hidden_pair_quantised_in(s))
             if unit_exists(s + 3):
                 group_hidden(s + 3)
-            if tile_exists(s + 6):
-                group_tokens(s + 6)
+            for i in tiles_turned_in(s):
+                group_tokens(i)
 
         work_of_slot(-6)
         work_of_slot(-5)

from contextlib import ExitStack

import concourse.mybir as mybir
from concourse.masks import make_identity

F32 = mybir.dt.float32
BF16 = mybir.dt.bfloat16
I32 = mybir.dt.int32
U32 = mybir.dt.uint32
U8 = mybir.dt.uint8
FP8X4 = mybir.dt.float8_e4m3fn_x4
ALU = mybir.AluOpType
ACT = mybir.ActivationFunctionType

P = 128
PACK = 4
K_PASS = P * PACK
FEATURES = 1024
TOKENS = 2 * 32 * 32
TILES = TOKENS // P
PASSES = FEATURES // K_PASS
BANK = 512
HALVES = FEATURES // BANK
PAIR = 2
PAIR_TOKENS = PAIR * P
PAIRS = TILES // PAIR
UNITS = PAIRS * PASSES
EPS = 1e-5
GAIN_ROWS = (0, 2, 3)
SHIFT_ROW = 4
BIAS_ROW = 32
LATE_WARMING_MATMULS = {TILES - 3: 2}
WARMING_MATMULS = 4
LATE_TILES = 4
BORROWED = 9

FLOPS = 2 * 2 * TOKENS * FEATURES * FEATURES


def tile_edgefeaturenet_pb_kernel(
    tc, h1, edge_mask, W2_words, W2_scales, b2, W3_words, W3_scales, b3, ln_g, ln_b, out
):
    nc = tc.nc
    h1_rows = h1.rearrange("b n (h i) k -> (b n h) i k", i=TILES)
    mask_rows = edge_mask.rearrange("b n (h i) -> (b n h) i", i=TILES)
    out_rows = out.rearrange("b n (h i) k -> (b n h) i k", i=TILES)

    with ExitStack() as stack:
        stack.enter_context(tc.manual_schedule())
        keep = stack.enter_context(tc.tile_pool(name="keep", bufs=1))
        stage = stack.enter_context(tc.tile_pool(name="stage", bufs=4))
        rows = stack.enter_context(tc.tile_pool(name="rows", bufs=4))
        stats = stack.enter_context(tc.tile_pool(name="stats", bufs=4))
        handover = stack.enter_context(tc.tile_pool(name="handover", bufs=4))
        psum_x = stack.enter_context(tc.psum_pool(name="psum_x", bufs=1))
        psum_h = stack.enter_context(tc.psum_pool(name="psum_h", bufs=2))
        psum_acc = stack.enter_context(tc.psum_pool(name="psum_acc", bufs=2))
        psum_rank = stack.enter_context(tc.psum_pool(name="psum_rank", bufs=2))
        psum_coef = stack.enter_context(tc.psum_pool(name="psum_coef", bufs=1))

        zeros = keep.tile([P, BANK], BF16, name="zeros")
        nc.gpsimd.memset(zeros[:], 0.0)

        def warm_tensor_engine(count):
            for dummy in range(count):
                idle_bank = psum_acc.tile([P, BANK], F32, name="acc")
                nc.tensor.matmul(out=idle_bank[:], lhsT=zeros[:, 0:P], rhs=zeros[:], start=True, stop=True)

        h1_sb = keep.tile([P, TILES, FEATURES], BF16, name="h1_sb")
        w2_words = [
            keep.tile([P, PASSES, BANK], U32, align_bytes=64, name="w2_words_0"),
            keep.tile([P, PASSES, BANK], U32, align_bytes=64, name="w2_words_1"),
        ]
        w3_words = keep.tile([P, PASSES, FEATURES], U32, align_bytes=64, name="w3_words")
        w2_planes = keep.tile([P, FEATURES], U8, align_bytes=64, name="w2_planes")
        nc.vector.memset(w2_planes[:].bitcast(I32), 0)
        w3_planes = keep.tile([P, FEATURES], U8, align_bytes=64, name="w3_planes")
        nc.vector.memset(w3_planes[:].bitcast(I32), 0)
        vec_rows = keep.tile([P, FEATURES], BF16, name="vec_rows")
        nc.vector.memset(vec_rows[:], 0.0)
        mask_bf16 = keep.tile([P, TILES], BF16, name="mask_bf16")
        b2_bf16 = keep.tile([P, PASSES, PACK], BF16, name="b2_bf16")

        def load_tokens(first_tile, end_tile):
            nc.sync.dma_start(out=h1_sb[:, first_tile:end_tile, :], in_=h1_rows[:, first_tile:end_tile, :])

        def load_scales(planes, scales):
            for quadrant in range(4):
                first = 32 * quadrant
                nc.sync.dma_start(
                    out=planes[first : first + 4 * PASSES, :].bitcast(I32),
                    in_=scales[:, 4 * quadrant : 4 * quadrant + 4, :].bitcast(I32),
                )

        def load_words(words_sb, words):
            by_partition = words.rearrange("g p n t -> p g (n t)")
            for n in range(HALVES):
                nc.sync.dma_start(
                    out=words_sb[:, :, n * BANK : (n + 1) * BANK].bitcast(I32),
                    in_=by_partition[:, :, n * BANK * PACK : (n + 1) * BANK * PACK].bitcast(I32),
                )

        def load_vector(row, vec):
            nc.sync.dma_start(out=vec_rows[row : row + 1, :], in_=vec.rearrange("(o n) -> o n", o=1))

        load_tokens(0, 1)
        load_tokens(1, 2)
        load_scales(w2_planes, W2_scales)
        nc.sync.dma_start(out=b2_bf16[:], in_=b2.rearrange("(a p t) -> p a t", a=PASSES, t=PACK))
        w2_by_partition = W2_words.rearrange("g p n t -> p g (n t)")
        for n in range(HALVES):
            nc.sync.dma_start(
                out=w2_words[n][:].bitcast(I32),
                in_=w2_by_partition[:, :, n * BANK * PACK : (n + 1) * BANK * PACK].bitcast(I32),
            )
        load_tokens(2, 4)
        load_vector(BIAS_ROW, b3)
        for row in GAIN_ROWS:
            load_vector(row, ln_g)
        load_vector(SHIFT_ROW, ln_b)
        nc.sync.dma_start(out=mask_bf16[:], in_=mask_rows)
        load_scales(w3_planes, W3_scales)
        load_tokens(4, 6)
        load_words(w3_words, W3_words)
        load_tokens(6, 7)
        load_tokens(7, 10)
        load_tokens(10, TILES)

        ident_f32 = keep.tile([P, P], F32, name="ident_f32")
        make_identity(nc, ident_f32[:])
        ident_bf16 = keep.tile([P, P], BF16, name="ident_bf16")
        make_identity(nc, ident_bf16[:])
        eps = keep.tile([P, 1], F32, name="eps")
        nc.vector.memset(eps[:], EPS)
        warm = keep.tile([P, 1], F32, name="warm")
        nc.scalar.activation(out=warm[:], in_=eps[:], func=ACT.Abs_reciprocal_sqrt)

        b2_cols = keep.tile([P, PASSES * PACK], F32, name="b2_cols")
        b3_all = keep.tile([P, FEATURES], BF16, name="b3_all")
        gain_all = keep.tile([P, FEATURES], BF16, name="gain_all")
        coef = keep.tile([P, TILES, P], BF16, name="coef")
        nc.vector.memset(coef[:], 0.0)
        port_value = keep.tile([P, 1], F32, name="port_value")
        mask = keep.tile([P, TILES], F32, name="mask")

        w2_sorted = keep.tile([P, PASSES, PASSES * PACK, P], U32, align_bytes=64, name="w2_sorted")
        w2_planes_sorted = keep.tile([P, FEATURES], U8, align_bytes=64, name="w2_planes_sorted")

        def sort_scales():
            nc.vector.tensor_copy(
                out=w2_planes_sorted[:].rearrange("p (a t m) -> p a m t", a=PASSES, t=PACK),
                in_=w2_planes[:].rearrange("p (a m t) -> p a m t", a=PASSES, t=PACK),
            )

        def sort_words(a):
            nc.vector.tensor_copy(
                out=w2_sorted[:, :, PACK * a : PACK * (a + 1), :].bitcast(I32),
                in_=w2_words[a][:].bitcast(I32).rearrange("p g (m t) -> p g t m", t=PACK),
            )

        def spread_vector(row, spread):
            for n in range(HALVES):
                cols = slice(n * BANK, (n + 1) * BANK)
                acc = psum_acc.tile([P, BANK], F32, name="acc")
                nc.tensor.matmul(
                    out=acc[:],
                    lhsT=ident_bf16[:, row : row + 1].to_broadcast([P, P]),
                    rhs=vec_rows[:, cols],
                    start=True,
                    stop=True,
                )
                if n == 0:
                    nc.vector.tensor_copy(out=spread[:, cols], in_=acc[:])
                else:
                    nc.scalar.copy(out=spread[:, cols], in_=acc[:])

        xt, x_grouped, x_mx, h_banks, h_planes, h_grouped, h_mx = {}, {}, {}, {}, {}, {}, {}
        y_banks, y, sums, neg_mean, sum_sq, rstd, mean_and_variance = {}, {}, {}, {}, {}, {}, {}
        slope, offset, rest, gained, coef_bank, coef_rows, rank_banks, results = {}, {}, {}, {}, {}, {}, {}, {}

        def transpose_tokens(i):
            pairs = h1_sb[:, i, :].bitcast(F32)
            if i < BORROWED and i % 3 != 0:
                xt[i] = psum_rank.tile([P, PASSES, 2, P], F32, name="rank")
            else:
                xt[i] = psum_x.tile([P, PASSES, 2, P], F32, name="xt")
            for g in range(PASSES):
                for u in range(2):
                    nc.tensor.transpose(
                        xt[i][:, g, u, :], pairs[:, 256 * g + u : 256 * (g + 1) : 2], ident_f32[:]
                    )

        def group_tokens(i):
            q, j = divmod(i, PAIR)
            if j == 0:
                x_grouped[q] = stage.tile([P, PASSES, PAIR_TOKENS, PACK], BF16, align_bytes=64, name="x_grouped")
            nc.scalar.copy(
                out=x_grouped[q][:, :, j * P : (j + 1) * P, :].bitcast(F32),
                in_=xt[i][:].rearrange("p g u r -> p g r u"),
            )

        def quantise(grouped_flat, width, tag):
            codes = stage.tile([P, width], U32, align_bytes=64, name="codes" + tag)
            scales = stage.tile([P, width], U8, align_bytes=64, name="scales" + tag)
            nc.vector.quantize_mx(out=codes[:].bitcast(FP8X4), scales=scales[:], in_=grouped_flat)
            return codes, scales

        def quantise_tokens(q):
            x_mx[q] = quantise(x_grouped[q][:].rearrange("p g r t -> p (g r t)"), PASSES * PAIR_TOKENS, "_x")

        def multiply_first(unit):
            q, a = divmod(unit, PASSES)
            codes, scales = x_mx[q]
            h_banks[unit] = []
            for half in range(2):
                bank = psum_h.tile([P, 2, PAIR_TOKENS], F32, name="hb")
                for e in range(2):
                    block = PACK * a + 2 * half + e
                    for g in range(PASSES):
                        tokens = slice(g * PAIR_TOKENS, (g + 1) * PAIR_TOKENS)
                        nc.tensor.matmul_mx(
                            out=bank[:, e, :],
                            lhsT=w2_sorted[:, g, block, :].bitcast(FP8X4),
                            lhsT_scale=w2_planes_sorted[4 * g : P, block * P : (block + 1) * P],
                            rhs=codes[:, tokens].bitcast(FP8X4),
                            rhs_scale=scales[:, tokens],
                            start=(g == 0),
                            stop=(g == PASSES - 1),
                        )
                h_banks[unit].append(bank)

        def bias_and_relu(unit, t):
            a = unit % PASSES
            if t == 0:
                h_planes[unit] = stage.tile([P, PACK, PAIR_TOKENS], BF16, name="h_planes")
            nc.scalar.activation(
                out=h_planes[unit][:, t, :],
                in_=h_banks[unit][t // 2][:, t % 2, :],
                func=ACT.Relu,
                bias=b2_cols[:, PACK * a + t : PACK * a + t + 1],
                scale=1.0,
            )

        def group_hidden(unit):
            q, a = divmod(unit, PASSES)
            if a == 0:
                h_grouped[q] = stage.tile([P, PASSES, PAIR_TOKENS, PACK], BF16, align_bytes=64, name="h_grouped")
            nc.vector.tensor_copy(
                out=h_grouped[q][:, a, :, :].rearrange("p (c i) t -> p c t i", i=4),
                in_=h_planes[unit][:].rearrange("p t (c i) -> p c t i", i=4),
            )

        def quantise_hidden(q):
            h_mx[q] = quantise(h_grouped[q][:].rearrange("p a r t -> p (a r t)"), PASSES * PAIR_TOKENS, "_h")

        def multiply_second(i):
            q, j = divmod(i, PAIR)
            codes, scales = h_mx[q]
            y_banks[i] = []
            for n in range(HALVES):
                cols = slice(n * BANK, (n + 1) * BANK)
                acc = psum_acc.tile([P, BANK], F32, name="acc")
                for a in range(PASSES):
                    tokens = slice(a * PAIR_TOKENS + j * P, a * PAIR_TOKENS + (j + 1) * P)
                    nc.tensor.matmul_mx(
                        out=acc[:],
                        lhsT=codes[:, tokens].bitcast(FP8X4),
                        lhsT_scale=scales[:, tokens],
                        rhs=w3_words[:, a, cols].bitcast(FP8X4),
                        rhs_scale=w3_planes[4 * a : P, cols],
                        start=(a == 0),
                        stop=(a == PASSES - 1),
                    )
                y_banks[i].append(acc)

        def add_bias_and_sum(i):
            y[i] = rows.tile([P, FEATURES], F32, name="y")
            sums[i] = stats.tile([P, HALVES], F32, name="sums")
            for n in range(HALVES):
                cols = slice(n * BANK, (n + 1) * BANK)
                nc.vector.scalar_tensor_tensor(
                    out=y[i][:, cols],
                    in0=y_banks[i][n][:],
                    scalar=1.0,
                    in1=b3_all[:, cols],
                    op0=ALU.mult,
                    op1=ALU.add,
                    accum_out=sums[i][:, n : n + 1] if i < TILES - 1 else None,
                )

        def statistics_on_vector(i):
            partial = stats.tile([P, HALVES, 6], F32, name="partial")
            for n in range(HALVES):
                nc.vector.bn_stats(out=partial[:, n, :], in_=y[i][:, n * BANK : (n + 1) * BANK])
            mean_and_variance[i] = stats.tile([P, 2], F32, name="mean_and_variance")
            nc.vector.bn_aggr(out=mean_and_variance[i][:], in_=partial[:].rearrange("p n c -> p (n c)"))
            neg_mean[i] = stats.tile([P, 1], F32, name="neg_mean")
            nc.vector.tensor_scalar(
                out=neg_mean[i][:], in0=mean_and_variance[i][:, 0:1], scalar1=-1.0, scalar2=None, op0=ALU.mult
            )

        def mean(i):
            neg_mean[i] = stats.tile([P, 1], F32, name="neg_mean")
            scaled = stats.tile([P, HALVES], F32, name="scaled")
            nc.scalar.activation(
                out=scaled[:], in_=sums[i][:], func=ACT.Identity, scale=-1.0 / FEATURES, accum_out=neg_mean[i][:]
            )

        def sum_squares(i):
            squares = rows.tile([P, FEATURES], BF16, name="squares")
            sum_sq[i] = stats.tile([P, 1], F32, name="sum_sq")
            nc.scalar.activation(
                out=squares[:],
                in_=y[i][:],
                func=ACT.Square,
                bias=neg_mean[i][:, 0:1],
                scale=1.0,
                accum_out=sum_sq[i][:],
            )

        def inverse_deviation(i):
            rstd[i] = stats.tile([P, 1], F32, name="rstd")
            if i == TILES - 1:
                nc.scalar.activation(
                    out=rstd[i][:],
                    in_=mean_and_variance[i][:, 1:2],
                    func=ACT.Abs_reciprocal_sqrt,
                    bias=eps[:, 0:1],
                    scale=1.0,
                )
            else:
                nc.scalar.activation(
                    out=rstd[i][:],
                    in_=sum_sq[i][:],
                    func=ACT.Abs_reciprocal_sqrt,
                    bias=eps[:, 0:1],
                    scale=1.0 / FEATURES,
                )

        def make_slope(i):
            slope[i] = stats.tile([P, 1], F32, name="slope")
            nc.scalar.activation(out=slope[i][:], in_=rstd[i][:], func=ACT.Identity, scale=mask[:, i : i + 1])

        def piece(i, number):
            return coef[:, i, GAIN_ROWS[number] : GAIN_ROWS[number] + 1]

        def make_offset(i):
            offset[i] = stats.tile([P, 1], F32, name="offset")
            nc.scalar.activation(out=offset[i][:], in_=neg_mean[i][:], func=ACT.Identity, scale=slope[i][:, 0:1])
            nc.scalar.activation(out=piece(i, 0), in_=neg_mean[i][:], func=ACT.Identity, scale=slope[i][:, 0:1])

        def second_piece(i):
            rest[i] = stats.tile([P, 1], F32, name="rest")
            nc.scalar.activation(out=rest[i][:], in_=piece(i, 0), func=ACT.Identity, bias=offset[i][:, 0:1], scale=-1.0)
            nc.scalar.activation(out=piece(i, 1), in_=piece(i, 0), func=ACT.Identity, bias=offset[i][:, 0:1], scale=-1.0)

        def third_piece(i):
            nc.scalar.activation(out=piece(i, 2), in_=piece(i, 1), func=ACT.Identity, bias=rest[i][:, 0:1], scale=-1.0)

        def turn_coefficients(i):
            coef_bank[i] = psum_coef.tile([P, P], F32, name="coef_bank")
            nc.tensor.matmul(out=coef_bank[i][:], lhsT=coef[:, i, :], rhs=ident_bf16[:], start=True, stop=True)

        def copy_coefficients(i):
            coef_rows[i] = stage.tile([P, P], BF16, name="coef_rows")
            nc.scalar.copy(out=coef_rows[i][:], in_=coef_bank[i][:])

        def outer_products(i):
            rank_banks[i] = []
            for n in range(HALVES):
                if i == TILES - 3:
                    bank = psum_h.tile([P, BANK], F32, name="hb")
                elif i == TILES - 1:
                    bank = psum_acc.tile([P, BANK], F32, name="acc")
                else:
                    bank = psum_rank.tile([P, BANK], F32, name="rank")
                nc.tensor.matmul(
                    out=bank[:], lhsT=coef_rows[i][:], rhs=vec_rows[:, n * BANK : (n + 1) * BANK], start=True, stop=True
                )
                rank_banks[i].append(bank)

        def gain(i, s):
            before = s - 1
            if unit_exists(before + 3):
                if tile_exists(before - 4):
                    nc.gpsimd.tensor_copy(out=port_value[:], in_=results[before - 4][:, FEATURES - 1 : FEATURES])
                else:
                    nc.gpsimd.tensor_copy(out=port_value[:], in_=sums[before - 1][:, HALVES - 1 : HALVES])
            gained[i] = handover.tile([P, FEATURES], F32, name="gained")
            nc.gpsimd.tensor_tensor(out=gained[i][:], in0=y[i][:], in1=gain_all[:], op=ALU.mult)

        def scale_shift_and_store(i):
            result = rows.tile([P, FEATURES], F32, name="result")
            results[i] = result
            pieces_of_bank = 2 if i == TILES - 1 else 1
            width = BANK // pieces_of_bank
            for n in range(HALVES):
                for piece_number in range(pieces_of_bank):
                    in_bank = slice(piece_number * width, (piece_number + 1) * width)
                    cols = slice(n * BANK + piece_number * width, n * BANK + (piece_number + 1) * width)
                    nc.vector.scalar_tensor_tensor(
                        out=result[:, cols],
                        in0=gained[i][:, cols],
                        scalar=slope[i][:, 0:1],
                        in1=rank_banks[i][n][:, in_bank],
                        op0=ALU.mult,
                        op1=ALU.add,
                    )
                    if i >= TILES - LATE_TILES:
                        nc.sync.dma_start(out=out_rows[:, i, cols], in_=result[:, cols])
            if i < TILES - LATE_TILES:
                nc.sync.dma_start(out=out_rows[:, i, :], in_=result[:])

        def tile_exists(i):
            return 0 <= i < TILES

        def unit_exists(unit):
            return 0 <= unit < UNITS

        def tiles_turned_in(s):
            if s == -4:
                return []
            if s == -3:
                return [2, 3]
            return [s + 6] if tile_exists(s + 6) else []

        def hidden_pair_quantised_in(s):
            q, odd = divmod(s + 1, PAIR)
            return q if odd == 0 and 0 <= q < PAIRS else None

        def pair_quantised_in(s):
            q, odd = divmod(s + 4, PAIR)
            return q if odd == 0 and 0 <= q < PAIRS else None

        def work_of_slot(s):
            if tile_exists(s - 3):
                turn_coefficients(s - 3)
            if unit_exists(s + 3):
                multiply_first(s + 3)
            for i in tiles_turned_in(s):
                transpose_tokens(i)
            if tile_exists(s - 2) and s - 2 < TILES - 1:
                sum_squares(s - 2)
            if s - 2 == TILES - 1:
                inverse_deviation(s - 2)
                make_slope(s - 2)
            if tile_exists(s - 1):
                add_bias_and_sum(s - 1)
            if s - 1 == TILES - 1:
                statistics_on_vector(s - 1)
            if tile_exists(s):
                multiply_second(s)
            if tile_exists(s - 4):
                scale_shift_and_store(s - 4)
            if tile_exists(s - 3):
                copy_coefficients(s - 3)
                outer_products(s - 3)
                warm_tensor_engine(LATE_WARMING_MATMULS.get(s - 3, 0))
            if tile_exists(s - 2):
                gain(s - 2, s)
            if unit_exists(s + 3):
                bias_and_relu(s + 3, 0)
            if tile_exists(s - 2) and s - 2 < TILES - 1:
                inverse_deviation(s - 2)
            if unit_exists(s + 3):
                bias_and_relu(s + 3, 1)
            if tile_exists(s - 2) and s - 2 < TILES - 1:
                make_slope(s - 2)
            if unit_exists(s + 3):
                bias_and_relu(s + 3, 2)
            if tile_exists(s - 2):
                make_offset(s - 2)
            if unit_exists(s + 3):
                bias_and_relu(s + 3, 3)
            if tile_exists(s - 2):
                second_piece(s - 2)
            if tile_exists(s - 1) and s - 1 < TILES - 1:
                mean(s - 1)
            if tile_exists(s - 2):
                third_piece(s - 2)
            if pair_quantised_in(s) is not None:
                quantise_tokens(pair_quantised_in(s))
            if hidden_pair_quantised_in(s) is not None:
                quantise_hidden(hidden_pair_quantised_in(s))
            if unit_exists(s + 3):
                group_hidden(s + 3)
            for i in tiles_turned_in(s):
                group_tokens(i)

        work_of_slot(-6)
        work_of_slot(-5)
        warm_tensor_engine(WARMING_MATMULS)
        nc.vector.tensor_copy(out=b2_cols[:], in_=b2_bf16[:].rearrange("p a t -> p (a t)"))
        sort_scales()
        sort_words(0)
        work_of_slot(-4)
        sort_words(1)
        work_of_slot(-3)
        nc.vector.tensor_copy(out=mask[:], in_=mask_bf16[:])
        nc.vector.tensor_copy(
            out=coef[:, :, SHIFT_ROW : SHIFT_ROW + 1], in_=mask_bf16[:].rearrange("p (i o) -> p i o", o=1)
        )
        work_of_slot(-2)
        spread_vector(BIAS_ROW, b3_all)
        work_of_slot(-1)
        spread_vector(GAIN_ROWS[0], gain_all)
        for s in range(0, TILES + 5):
            work_of_slot(s)
